import numpy as np
import ml_dtypes


def mxq(x, axis, fmt="e4m3"):
    dtype, down = {"e4m3": (ml_dtypes.float8_e4m3fn, 7), "e5m2": (ml_dtypes.float8_e5m2, 14)}[fmt]
    v = np.moveaxis(np.asarray(x, np.float32).astype(ml_dtypes.bfloat16).astype(np.float64), axis, -1)
    blocks = v.reshape(v.shape[:-1] + (-1, 32))
    amax = np.abs(blocks).max(-1, keepdims=True)
    byte = np.maximum(np.where(amax > 0, np.frexp(amax)[1] - 1 + 127, 0) - down, 1)
    scale = np.exp2(byte - 127.0)
    codes = (blocks / scale).astype(np.float32).astype(dtype).astype(np.float64)
    return np.moveaxis((codes * scale).reshape(v.shape), -1, axis)


WIDE = False


def mx_kscale(k):
    if not WIDE:
        return np.ones(k)
    levels = np.array([10, -10, 5, -5, 0])
    a = np.random.permutation(np.resize(levels, k // 512 * 4)).reshape(k // 512, 4)
    idx = np.arange(k)
    return np.exp2(a[idx // 512, idx % 128 // 32])


BF16 = ml_dtypes.bfloat16


def bf(x):
    return np.asarray(x, np.float32).astype(BF16)


def f64(x):
    return np.asarray(x).astype(np.float64)


B, I, J, P, D = 32, 512, 512, 32, 4
EPS = 1e-5


def stdz(t):
    m = t.mean(axis=(-1, -2), keepdims=True)
    s = t.std(axis=(-1, -2), keepdims=True, ddof=1)
    return (t - m) / (s + EPS)


def flat_softmax(t):
    e = np.exp(t - t.max(axis=(-1, -2), keepdims=True))
    return e / e.sum(axis=(-1, -2), keepdims=True)


def setup_inputs():
    s = mx_kscale(J)
    return {"x": bf((np.random.standard_normal((B, I, J)) + 0.25) * s),
            "o_xj": bf((np.random.standard_normal((D, J, P)) * 2.0 / np.sqrt(J + P) + 2.0 / J) / s[:, None]),
            "p_xj": bf(np.random.standard_normal((D, I, P)) * 2.0 / np.sqrt(I + P)),
            "rel_o_xj": bf(np.random.standard_normal((D, J, P)) * 2.0 / np.sqrt(J + P) / s[:, None])}


def reference(x, o_xj, p_xj, rel_o_xj):
    xq = mxq(f64(x), 2, "e4m3")[:, None]
    mass = flat_softmax(xq @ mxq(f64(rel_o_xj), 1, "e4m3")).sum(-2)
    t = stdz(np.tanh(xq @ mxq(f64(o_xj), 1, "e4m3")))
    u = mxq(t, 2, "e4m3").transpose(0, 1, 3, 2) @ mxq(f64(p_xj), 1, "e4m3")
    return stdz(np.tanh(u)), mass

@@ -1,0 +1,449 @@
+from contextlib import ExitStack
+
+import concourse.mybir as mybir
+from concourse.masks import make_identity
+
+F32 = mybir.dt.float32
+BF16 = mybir.dt.bfloat16
+U32 = mybir.dt.uint32
+U8 = mybir.dt.uint8
+FP8X4 = mybir.dt.float8_e4m3fn_x4
+ACT = mybir.ActivationFunctionType
+ALU = mybir.AluOpType
+AX = mybir.AxisListType
+
+NB = 32
+ND = 4
+NI = 512
+NJ = 512
+NP = 32
+P = 128
+EPS = 1e-5
+FLOPS = 2 * NB * ND * (2 * NI * NJ * NP + NP * NI * NP)
+
+PIN = True
+LAG = 6
+FIRST = 5
+XRING = 10
+NG = NB // 4
+
+
+def tile_selfprojectiondev_pa_t_kernel(tc, x, o_xj, p_xj, rel_o_xj, out_0, out_1):
+    nc = tc.nc
+    with ExitStack() as ctx:
+        const = ctx.enter_context(tc.tile_pool(name="const", bufs=1))
+        xpool = ctx.enter_context(tc.tile_pool(name="xpool", bufs=XRING))
+        gpool = ctx.enter_context(tc.tile_pool(name="gpool", bufs=3))
+        cpool = ctx.enter_context(tc.tile_pool(name="cpool", bufs=LAG + 1))
+        thpool = ctx.enter_context(tc.tile_pool(name="thpool", bufs=3))
+        stpool = ctx.enter_context(tc.tile_pool(name="stpool", bufs=2))
+        mepool = ctx.enter_context(tc.tile_pool(name="mepool", bufs=5))
+        tgpool = ctx.enter_context(tc.tile_pool(name="tgpool", bufs=2))
+        vpool = ctx.enter_context(tc.tile_pool(name="vpool", bufs=5))
+        jpool = ctx.enter_context(tc.tile_pool(name="jpool", bufs=2))
+        ps_xt = ctx.enter_context(tc.psum_pool(name="ps_xt", bufs=3))
+        ps_z = ctx.enter_context(tc.psum_pool(name="ps_z", bufs=1))
+        ps_r = ctx.enter_context(tc.psum_pool(name="ps_r", bufs=2))
+        ps_st = ctx.enter_context(tc.psum_pool(name="ps_st", bufs=1))
+        ps_u = ctx.enter_context(tc.psum_pool(name="ps_u", bufs=1))
+        if PIN:
+            ctx.enter_context(tc.manual_schedule())
+
+        ident = const.tile([P, P], F32, name="ident")
+        make_identity(nc, ident[:])
+        ones256 = const.tile([P, P], F32, name="ones256")
+        nc.vector.memset(ones256[:], 1.0 / 256.0)
+        ones16k = const.tile([P, P], F32, name="ones16k")
+        nc.vector.memset(ones16k[:], 1.0 / 16384.0)
+        bd1024 = const.tile([P, P], F32, name="bd1024")
+        nc.vector.memset(bd1024[:], 0.0)
+        for q in range(4):
+            nc.vector.memset(bd1024[32 * q : 32 * q + 32, 32 * q : 32 * q + 32], 1.0 / 1024.0)
+        half = const.tile([P, 24], F32, name="half")
+        nc.vector.memset(half[:], 0.5)
+        negmax = const.tile([P, P], F32, name="negmax")
+        nc.vector.memset(negmax[:], 0.0)
+        expsum = const.tile([P, P], F32, name="expsum")
+        nc.vector.memset(expsum[:], 0.0)
+
+        xs = {}
+
+        def load_pair(k, split):
+            t = xpool.tile([P, 2, 4, NJ], BF16, name="xs", tag="xs")
+            xs[k] = t
+            if split:
+                for bi in range(2):
+                    nc.sync.dma_start(
+                        out=t[:, bi].rearrange("q c j -> q (c j)"),
+                        in_=x[2 * k + bi].rearrange("(q c) j -> q (c j)", c=4),
+                    )
+            else:
+                nc.sync.dma_start(
+                    out=t[:].rearrange("q b c j -> q b (c j)"),
+                    in_=x[2 * k : 2 * k + 2].rearrange("b (q c) j -> q b (c j)", c=4),
+                )
+
+        load_pair(0, True)
+
+        wraw = const.tile([P, 3, ND, 4, NP], BF16, name="wraw")
+        for kind, w in ((0, o_xj), (1, rel_o_xj)):
+            wv = w.rearrange("d (u p e) n -> u p d (e n)", u=2, p=P, e=2)
+            for u in range(2):
+                nc.scalar.dma_start(
+                    out=wraw[:, kind, :, 2 * u : 2 * u + 2, :].rearrange("p d e n -> p d (e n)"),
+                    in_=wv[u],
+                )
+        nc.scalar.dma_start(
+            out=wraw[:, 2].rearrange("q d c n -> q d (c n)"),
+            in_=p_xj.rearrange("d (q c) n -> q d (c n)", c=4),
+        )
+        for k in range(1, XRING):
+            load_pair(k, False)
+
+        wgrp = const.tile([P, 3, P, 4], BF16, name="wgrp", align_bytes=64)
+        wcod = const.tile([P, 3 * P], U32, name="wcod", align_bytes=64)
+        wsc = const.tile([P, 3 * P], U8, name="wsc", align_bytes=64)
+        nc.vector.tensor_copy(
+            out=wgrp[:, 0:2].rearrange("p k (d n) t -> p (k d) n t", d=ND),
+            in_=wraw[:, 0:2].rearrange("p k d t n -> p (k d) n t"),
+        )
+        nc.vector.tensor_copy(
+            out=wgrp[:, 2].rearrange("p (d n) t -> p d n t", d=ND),
+            in_=wraw[:, 2].rearrange("p d t n -> p d n t"),
+        )
+        nc.vector.quantize_mx(
+            out=wcod[:, 0 : 2 * P].bitcast(FP8X4),
+            scales=wsc[:, 0 : 2 * P],
+            in_=wgrp[:, 0:2].rearrange("p k w t -> p (k w t)"),
+        )
+        nc.vector.quantize_mx(
+            out=wcod[:, 2 * P : 3 * P].bitcast(FP8X4),
+            scales=wsc[:, 2 * P : 3 * P],
+            in_=wgrp[:, 2].rearrange("p w t -> p (w t)"),
+        )
+
+        def wslice(kind):
+            return (
+                wcod[:, kind * P : (kind + 1) * P].bitcast(FP8X4),
+                wsc[:, kind * P : (kind + 1) * P],
+            )
+
+        xt = {}
+        grp = {}
+        xc = {}
+        zt = {}
+        rt = {}
+        th = {}
+        st = {}
+
+        def transposes(b):
+            pair = xs[b // 2]
+            banks = []
+            for h in range(2):
+                bank = ps_xt.tile([P, 2, 256], F32, name="xtb", tag="xtb")
+                for cc in range(2):
+                    xw = pair[:, b % 2, 2 * h + cc, :].bitcast(F32)
+                    for u in range(2):
+                        nc.tensor.transpose(
+                            bank[:, u, cc * P : (cc + 1) * P], xw[:, u * P : (u + 1) * P], ident[:]
+                        )
+                banks.append(bank)
+            xt[b] = banks
+
+        def evacuate(b):
+            g = gpool.tile([P, 4 * NI], BF16, name="grp", tag="grp", align_bytes=64)
+            grp[b] = g
+            g32 = g[:].bitcast(F32)
+            for h in range(2):
+                nc.scalar.copy(
+                    out=g32[:, h * 512 : (h + 1) * 512].rearrange("p (i u) -> p i u", u=2),
+                    in_=xt[b][h][:].rearrange("p u i -> p i u"),
+                )
+
+        def quantise_x(b):
+            cod = cpool.tile([P, NI], U32, name="xcod", tag="xcod", align_bytes=64)
+            sc = cpool.tile([P, NI], U8, name="xsc", tag="xsc", align_bytes=64)
+            xc[b] = (cod, sc)
+            nc.vector.quantize_mx(out=cod[:].bitcast(FP8X4), scales=sc[:], in_=grp[b][:])
+
+        def matmul_z(b):
+            cod, sc = xc[b]
+            z = ps_z.tile([P, 4, P], F32, name="zps", tag="zps")
+            zt[b] = z
+            wc, ws = wslice(0)
+            for c in range(4):
+                nc.tensor.matmul_mx(
+                    out=z[:, c, :],
+                    lhsT=cod[:, c * P : (c + 1) * P].bitcast(FP8X4),
+                    lhsT_scale=sc[:, c * P : (c + 1) * P],
+                    rhs=wc,
+                    rhs_scale=ws,
+                    start=True,
+                    stop=True,
+                )
+
+        def matmul_r(b):
+            cod, sc = xc[b]
+            r = ps_r.tile([P, NI], F32, name="rps", tag="rps")
+            rt[b] = r
+            wc, ws = wslice(1)
+            nc.tensor.matmul_mx(
+                out=r[:],
+                lhsT=wc,
+                lhsT_scale=ws,
+                rhs=cod[:].bitcast(FP8X4),
+                rhs_scale=sc[:],
+                start=True,
+                stop=True,
+            )
+
+        def row_max(b):
+            nc.vector.tensor_reduce(
+                out=negmax[:, b : b + 1], in_=rt[b][:], axis=AX.X, op=ALU.max, negate=True
+            )
+
+        def row_exp(b):
+            junk = jpool.tile([P, NI], BF16, name="junk", tag="junk")
+            nc.scalar.activation(
+                out=junk[:],
+                in_=rt[b][:],
+                func=ACT.Exp,
+                bias=negmax[:, b : b + 1],
+                scale=1.0,
+                accum_out=expsum[:, b : b + 1],
+            )
+
+        def tanh_z(b):
+            g, bl = b // 4, b % 4
+            if bl == 0:
+                th[g] = thpool.tile([P, 4, 512], F32, name="th", tag="th")
+            nc.scalar.activation(
+                out=th[g][:, bl, :].rearrange("p (w c) -> p w c", c=4),
+                in_=zt[b][:].rearrange("p c w -> p w c"),
+                func=ACT.Tanh,
+            )
+
+        def stats_z(b):
+            g, bl = b // 4, b % 4
+            if bl == 0:
+                st[g] = stpool.tile([P, 16, 6], F32, name="st", tag="st")
+            for d in range(ND):
+                nc.vector.bn_stats(
+                    out=st[g][:, bl * 4 + d, :], in_=th[g][:, bl, d * P : (d + 1) * P]
+                )
+
+        me = {}
+        wk = {}
+        rs = {}
+        tg = {}
+        tcd = {}
+        ups = {}
+        vv = {}
+        s12 = {}
+        stp = {}
+
+        def chain_tiles(key):
+            if key not in me:
+                me[key] = mepool.tile([P, 2, 24], F32, name="me", tag="me")
+                wk[key] = mepool.tile([P, 5, 24], F32, name="wk", tag="wk")
+                rs[key] = mepool.tile([P, 24], F32, name="rs", tag="rs")
+
+        def stats1_sum(g):
+            sv = st[g][:].rearrange("p k (h s) -> p k h s", s=3)
+            means = sv[:, :, :, 1]
+            m2s = sv[:, :, :, 2]
+            sqm = mepool.tile([P, 16, 2], F32, name="sqm", tag="sqm")
+            nc.gpsimd.tensor_tensor(out=sqm[:], in0=means, in1=means, op=ALU.mult)
+            ps = ps_st.tile([P, 2, 16, 2], F32, name="stps", tag="stps")
+            stp[g] = ps
+            nc.tensor.matmul(ps[:, 0], lhsT=ones256[:], rhs=means, start=True, stop=True)
+            nc.tensor.matmul(ps[:, 1], lhsT=ones16k[:], rhs=m2s, start=True, stop=False)
+            nc.tensor.matmul(ps[:, 1], lhsT=ones256[:], rhs=sqm[:], start=False, stop=True)
+
+        def stats1_out(g):
+            chain_tiles(g)
+            nc.vector.tensor_reduce(out=me[g][:, :, 0:16], in_=stp[g][:], axis=AX.X, op=ALU.add)
+
+        def chain(key, c0, c1):
+            m, w = me[key], wk[key]
+            nc.gpsimd.tensor_tensor(out=w[:, 0, c0:c1], in0=m[:, 0, c0:c1], in1=m[:, 0, c0:c1], op=ALU.mult)
+            nc.gpsimd.tensor_tensor(out=w[:, 1, c0:c1], in0=m[:, 1, c0:c1], in1=w[:, 0, c0:c1], op=ALU.subtract)
+            nc.gpsimd.tensor_scalar(
+                out=w[:, 2, c0:c1], in0=w[:, 1, c0:c1], scalar1=0.0, scalar2=None, op0=ALU.max
+            )
+            nc.gpsimd.tensor_tensor(out=w[:, 3, c0:c1], in0=w[:, 2, c0:c1], in1=half[:, c0:c1], op=ALU.pow)
+            if c0 < 16:
+                nc.gpsimd.tensor_scalar(
+                    out=w[:, 4, c0:16], in0=w[:, 3, c0:16],
+                    scalar1=(16384.0 / 16383.0) ** 0.5, scalar2=EPS, op0=ALU.mult, op1=ALU.add,
+                )
+            if c1 > 16:
+                a = max(c0, 16)
+                nc.gpsimd.tensor_scalar(
+                    out=w[:, 4, a:c1], in0=w[:, 3, a:c1],
+                    scalar1=(1024.0 / 1023.0) ** 0.5, scalar2=EPS, op0=ALU.mult, op1=ALU.add,
+                )
+
+        def recip(key, c0, c1):
+            nc.vector.reciprocal(out=rs[key][:, c0:c1], in_=wk[key][:, 4, c0:c1])
+
+        def standardise(g, bl):
+            if bl == 0:
+                tg[g] = tgpool.tile([P, 2048], BF16, name="tg", tag="tg", align_bytes=64)
+            for d in range(ND):
+                col = bl * 4 + d
+                nc.vector.tensor_scalar(
+                    out=tg[g][:, (d * 4 + bl) * P : (d * 4 + bl + 1) * P],
+                    in0=th[g][:, bl, d * P : (d + 1) * P],
+                    scalar1=me[g][:, 0, col : col + 1],
+                    scalar2=rs[g][:, col : col + 1],
+                    op0=ALU.subtract,
+                    op1=ALU.mult,
+                )
+
+        def quantise_t(g):
+            cod = tgpool.tile([P, 512], U32, name="tcod", tag="tcod", align_bytes=64)
+            sc = tgpool.tile([P, 512], U8, name="tsc", tag="tsc", align_bytes=64)
+            tcd[g] = (cod, sc)
+            nc.vector.quantize_mx(out=cod[:].bitcast(FP8X4), scales=sc[:], in_=tg[g][:])
+
+        def matmul_u(g):
+            cod, sc = tcd[g]
+            u = ps_u.tile([P, 16, NP], F32, name="ups", tag="ups")
+            ups[g] = u
+            wc, ws = wslice(2)
+            for d in range(ND):
+                nc.tensor.matmul_mx(
+                    out=u[:, 4 * d : 4 * d + 4, :].rearrange("p k q -> p (k q)"),
+                    lhsT=cod[:, d * P : (d + 1) * P].bitcast(FP8X4),
+                    lhsT_scale=sc[:, d * P : (d + 1) * P],
+                    rhs=wc,
+                    rhs_scale=ws,
+                    start=True,
+                    stop=True,
+                )
+
+        def tanh_u(g):
+            v = vpool.tile([P, 2, ND, NP], F32, name="vv", tag="vv")
+            vv[g] = v
+            nc.scalar.activation(out=v[:, 0], in_=ups[g][:, 0:16:5, :], func=ACT.Tanh)
+            nc.scalar.activation(out=v[:, 1], in_=v[:, 0], func=ACT.Square)
+
+        def stats2_sum(g):
+            s = vpool.tile([P, 8], F32, name="s12", tag="s12")
+            s12[g] = s
+            nc.vector.tensor_reduce(
+                out=s[:], in_=vv[g][:].rearrange("p k d q -> p (k d) q"), axis=AX.X, op=ALU.add
+            )
+            ps = ps_st.tile([P, 8], F32, name="stps2", tag="stps")
+            stp[("u", g)] = ps
+            nc.tensor.matmul(ps[:], lhsT=bd1024[:], rhs=s[:], start=True, stop=True)
+
+        def stats2_out(g, key, c0):
+            chain_tiles(key)
+            nc.vector.tensor_copy(
+                out=me[key][:, :, c0 : c0 + 4],
+                in_=stp[("u", g)][:].rearrange("p (k d) -> p k d", k=2),
+            )
+
+        def finish(g, key, c0):
+            ov = vpool.tile([P, ND, NP], F32, name="ov", tag="ov")
+            for d in range(ND):
+                nc.vector.tensor_scalar(
+                    out=ov[:, d, :],
+                    in0=vv[g][:, 0, d, :],
+                    scalar1=me[key][:, 0, c0 + d : c0 + d + 1],
+                    scalar2=rs[key][:, c0 + d : c0 + d + 1],
+                    op0=ALU.subtract,
+                    op1=ALU.mult,
+                )
+            for bl in range(4):
+                nc.sync.dma_start(
+                    out=out_0[4 * g + bl].rearrange("d n q -> n d q"),
+                    in_=ov[32 * bl : 32 * bl + 32, :, :],
+                )
+
+        def softmax_finish():
+            tp = ps_xt.tile([P, 2, P], F32, name="smps", tag="xtb")
+            nc.tensor.transpose(tp[:, 0, :], negmax[:], ident[:])
+            nc.tensor.transpose(tp[:, 1, :], expsum[:], ident[:])
+            nmt = tp[0:NB, 0, :].rearrange("b (d n) -> b d n", d=ND)
+            smt = tp[0:NB, 1, :].rearrange("b (d n) -> b d n", d=ND)
+            gmin = const.tile([NB, ND], F32, name="gmin")
+            nc.vector.tensor_reduce(out=gmin[:], in_=nmt, axis=AX.X, op=ALU.min)
+            diff = const.tile([NB, ND, NP], F32, name="diff")
+            nc.vector.tensor_tensor(
+                out=diff[:], in0=gmin[:].unsqueeze(2).to_broadcast([NB, ND, NP]), in1=nmt, op=ALU.subtract
+            )
+            ex = const.tile([NB, ND, NP], F32, name="ex")
+            nc.scalar.activation(out=ex[:], in_=diff[:], func=ACT.Exp)
+            wgt = const.tile([NB, ND, NP], F32, name="wgt")
+            nc.vector.tensor_tensor(out=wgt[:], in0=ex[:], in1=smt, op=ALU.mult)
+            tot = const.tile([NB, ND], F32, name="tot")
+            nc.vector.tensor_reduce(out=tot[:], in_=wgt[:], axis=AX.X, op=ALU.add)
+            rtot = const.tile([NB, ND], F32, name="rtot")
+            nc.vector.reciprocal(out=rtot[:], in_=tot[:])
+            mass = const.tile([NB, ND, NP], F32, name="mass")
+            nc.vector.tensor_tensor(
+                out=mass[:], in0=wgt[:], in1=rtot[:].unsqueeze(2).to_broadcast([NB, ND, NP]), op=ALU.mult
+            )
+            nc.sync.dma_start(out=out_1[:, :, :], in_=mass[:])
+
+        def due(step, offset, count):
+            g, rem = divmod(step - FIRST - offset, 4)
+            return g if rem == 0 and 0 <= g < count else None
+
+        transposes(0)
+        for s in range(FIRST + 4 * (NG + 2) + 6):
+            rb = s - LAG
+            if 0 <= s - 2 < NB:
+                tanh_z(s - 2)
+            if s < NB:
+                evacuate(s)
+            if 0 <= rb < NB:
+                row_max(rb)
+                row_exp(rb)
+            if 0 <= s - 1 < NB:
+                quantise_x(s - 1)
+            if 0 <= s - 2 < NB:
+                stats_z(s - 2)
+            if 0 <= rb + 1 < NB:
+                matmul_r(rb + 1)
+            if 0 <= s - 1 < NB:
+                matmul_z(s - 1)
+            if s + 1 < NB:
+                transposes(s + 1)
+                if s % 2 == 0 and (s + 1) // 2 + XRING < NB // 2:
+                    load_pair((s + 1) // 2 + XRING, False)
+            g = due(s, 12, NG)
+            if g is not None:
+                stats2_out(g, g + 3, 16)
+            g = due(s, 11, NG)
+            if g is not None:
+                stats2_sum(g)
+            g = due(s, 10, NG)
+            if g is not None:
+                tanh_u(g)
+            g = due(s, 9, NG)
+            if g is not None:
+                quantise_t(g)
+                matmul_u(g)
+            k = due(s, 5, NG + 3)
+            if k is not None:
+                recip(k, 0 if k < NG else 16, 20 if k >= 3 else 16)
+                if k >= 3:
+                    finish(k - 3, k, 16)
+            for bl in range(4):
+                g = due(s, 5 + bl, NG)
+                if g is not None:
+                    standardise(g, bl)
+            k = due(s, 1, NG + 3)
+            if k is not None:
+                if k < NG:
+                    stats1_out(k)
+                chain(k, 0 if k < NG else 16, 20 if k >= 3 else 16)
+            g = due(s, 0, NG)
+            if g is not None:
+                stats1_sum(g)
+            if rb == NB:
+                softmax_finish()

@@ -24,6 +24,7 @@ FLOPS = 2 * NB * ND * (2 * NI * NJ * NP + NP * NI * NP)
 PIN = True
 LAG = 6
 FIRST = 5
+DUP = 2
 XRING = 10
 NG = NB // 4
 
@@ -35,7 +36,7 @@ def tile_selfprojectiondev_pa_t_kernel(tc, x, o_xj, p_xj, rel_o_xj, out_0, out_1
         xpool = ctx.enter_context(tc.tile_pool(name="xpool", bufs=XRING))
         gpool = ctx.enter_context(tc.tile_pool(name="gpool", bufs=3))
         cpool = ctx.enter_context(tc.tile_pool(name="cpool", bufs=LAG + 1))
-        thpool = ctx.enter_context(tc.tile_pool(name="thpool", bufs=3))
+        thpool = ctx.enter_context(tc.tile_pool(name="thpool", bufs=4))
         stpool = ctx.enter_context(tc.tile_pool(name="stpool", bufs=2))
         mepool = ctx.enter_context(tc.tile_pool(name="mepool", bufs=5))
         tgpool = ctx.enter_context(tc.tile_pool(name="tgpool", bufs=2))
@@ -187,15 +188,16 @@ def tile_selfprojectiondev_pa_t_kernel(tc, x, o_xj, p_xj, rel_o_xj, out_0, out_1
             r = ps_r.tile([P, NI], F32, name="rps", tag="rps")
             rt[b] = r
             wc, ws = wslice(1)
-            nc.tensor.matmul_mx(
-                out=r[:],
-                lhsT=wc,
-                lhsT_scale=ws,
-                rhs=cod[:].bitcast(FP8X4),
-                rhs_scale=sc[:],
-                start=True,
-                stop=True,
-            )
+            for rep in range(DUP):
+                nc.tensor.matmul_mx(
+                    out=r[:],
+                    lhsT=wc,
+                    lhsT_scale=ws,
+                    rhs=cod[:].bitcast(FP8X4),
+                    rhs_scale=sc[:],
+                    start=True,
+                    stop=True,
+                )
 
         def row_max(b):
             nc.vector.tensor_reduce(
@@ -248,44 +250,60 @@ def tile_selfprojectiondev_pa_t_kernel(tc, x, o_xj, p_xj, rel_o_xj, out_0, out_1
                 wk[key] = mepool.tile([P, 5, 24], F32, name="wk", tag="wk")
                 rs[key] = mepool.tile([P, 24], F32, name="rs", tag="rs")
 
-        def stats1_sum(g):
+        sqms = {}
+
+        def square_means(g):
             sv = st[g][:].rearrange("p k (h s) -> p k h s", s=3)
-            means = sv[:, :, :, 1]
-            m2s = sv[:, :, :, 2]
             sqm = mepool.tile([P, 16, 2], F32, name="sqm", tag="sqm")
-            nc.gpsimd.tensor_tensor(out=sqm[:], in0=means, in1=means, op=ALU.mult)
+            sqms[g] = sqm
+            nc.scalar.activation(out=sqm[:], in_=sv[:, :, :, 1], func=ACT.Square)
+
+        def stats1_matmul(g):
+            sv = st[g][:].rearrange("p k (h s) -> p k h s", s=3)
             ps = ps_st.tile([P, 2, 16, 2], F32, name="stps", tag="stps")
             stp[g] = ps
-            nc.tensor.matmul(ps[:, 0], lhsT=ones256[:], rhs=means, start=True, stop=True)
-            nc.tensor.matmul(ps[:, 1], lhsT=ones16k[:], rhs=m2s, start=True, stop=False)
-            nc.tensor.matmul(ps[:, 1], lhsT=ones256[:], rhs=sqm[:], start=False, stop=True)
+            nc.tensor.matmul(ps[:, 0], lhsT=ones256[:], rhs=sv[:, :, :, 1], start=True, stop=True)
+            nc.tensor.matmul(ps[:, 1], lhsT=ones16k[:], rhs=sv[:, :, :, 2], start=True, stop=False)
+            nc.tensor.matmul(ps[:, 1], lhsT=ones256[:], rhs=sqms[g][:], start=False, stop=True)
 
         def stats1_out(g):
             chain_tiles(g)
             nc.vector.tensor_reduce(out=me[g][:, :, 0:16], in_=stp[g][:], axis=AX.X, op=ALU.add)
 
-        def chain(key, c0, c1):
-            m, w = me[key], wk[key]
-            nc.gpsimd.tensor_tensor(out=w[:, 0, c0:c1], in0=m[:, 0, c0:c1], in1=m[:, 0, c0:c1], op=ALU.mult)
-            nc.gpsimd.tensor_tensor(out=w[:, 1, c0:c1], in0=m[:, 1, c0:c1], in1=w[:, 0, c0:c1], op=ALU.subtract)
-            nc.gpsimd.tensor_scalar(
-                out=w[:, 2, c0:c1], in0=w[:, 1, c0:c1], scalar1=0.0, scalar2=None, op0=ALU.max
-            )
+        def cols(k):
+            return (0 if k < NG else 16), (20 if k >= 3 else 16)
+
+        def var_step(k, i):
+            c0, c1 = cols(k)
+            m, w = me[k], wk[k]
+            if i == 0:
+                nc.vector.tensor_tensor(out=w[:, 0, c0:c1], in0=m[:, 0, c0:c1], in1=m[:, 0, c0:c1], op=ALU.mult)
+            elif i == 1:
+                nc.vector.tensor_tensor(out=w[:, 1, c0:c1], in0=m[:, 1, c0:c1], in1=w[:, 0, c0:c1], op=ALU.max)
+            else:
+                nc.vector.tensor_tensor(out=w[:, 2, c0:c1], in0=w[:, 1, c0:c1], in1=w[:, 0, c0:c1], op=ALU.subtract)
+
+        def root(k):
+            c0, c1 = cols(k)
+            w = wk[k]
             nc.gpsimd.tensor_tensor(out=w[:, 3, c0:c1], in0=w[:, 2, c0:c1], in1=half[:, c0:c1], op=ALU.pow)
-            if c0 < 16:
-                nc.gpsimd.tensor_scalar(
-                    out=w[:, 4, c0:16], in0=w[:, 3, c0:16],
-                    scalar1=(16384.0 / 16383.0) ** 0.5, scalar2=EPS, op0=ALU.mult, op1=ALU.add,
+
+        def scale_std(k):
+            w = wk[k]
+            if k < NG:
+                nc.scalar.activation(
+                    out=w[:, 4, 0:16], in_=w[:, 3, 0:16], func=ACT.Copy,
+                    scale=(16384.0 / 16383.0) ** 0.5, bias=EPS,
                 )
-            if c1 > 16:
-                a = max(c0, 16)
-                nc.gpsimd.tensor_scalar(
-                    out=w[:, 4, a:c1], in0=w[:, 3, a:c1],
-                    scalar1=(1024.0 / 1023.0) ** 0.5, scalar2=EPS, op0=ALU.mult, op1=ALU.add,
+            if k >= 3:
+                nc.scalar.activation(
+                    out=w[:, 4, 16:20], in_=w[:, 3, 16:20], func=ACT.Copy,
+                    scale=(1024.0 / 1023.0) ** 0.5, bias=EPS,
                 )
 
-        def recip(key, c0, c1):
-            nc.vector.reciprocal(out=rs[key][:, c0:c1], in_=wk[key][:, 4, c0:c1])
+        def recip(k):
+            c0, c1 = cols(k)
+            nc.vector.reciprocal(out=rs[k][:, c0:c1], in_=wk[k][:, 4, c0:c1])
 
         def standardise(g, bl):
             if bl == 0:
@@ -341,7 +359,7 @@ def tile_selfprojectiondev_pa_t_kernel(tc, x, o_xj, p_xj, rel_o_xj, out_0, out_1
 
         def stats2_out(g, key, c0):
             chain_tiles(key)
-            nc.vector.tensor_copy(
+            nc.scalar.copy(
                 out=me[key][:, :, c0 : c0 + 4],
                 in_=stp[("u", g)][:].rearrange("p (k d) -> p k d", k=2),
             )
@@ -394,19 +412,37 @@ def tile_selfprojectiondev_pa_t_kernel(tc, x, o_xj, p_xj, rel_o_xj, out_0, out_1
             return g if rem == 0 and 0 <= g < count else None
 
         transposes(0)
-        for s in range(FIRST + 4 * (NG + 2) + 6):
+        for s in range(FIRST + 4 * (NG + 2) + 7):
             rb = s - LAG
+            kp = due(s, 2, NG + 3)
+            kf = due(s, 6, NG + 3)
+            g1 = due(s, 1, NG)
+            if kf is not None:
+                scale_std(kf)
             if 0 <= s - 2 < NB:
                 tanh_z(s - 2)
+            if g1 is not None:
+                square_means(g1)
+            g = due(s, 13, NG)
+            if g is not None:
+                stats2_out(g, g + 3, 16)
             if s < NB:
                 evacuate(s)
             if 0 <= rb < NB:
                 row_max(rb)
                 row_exp(rb)
+            if kp is not None and kp < NG:
+                stats1_out(kp)
+            if kf is not None:
+                recip(kf)
             if 0 <= s - 1 < NB:
                 quantise_x(s - 1)
+            if kp is not None:
+                var_step(kp, 0)
             if 0 <= s - 2 < NB:
                 stats_z(s - 2)
+            if kp is not None:
+                var_step(kp, 1)
             if 0 <= rb + 1 < NB:
                 matmul_r(rb + 1)
             if 0 <= s - 1 < NB:
@@ -415,35 +451,26 @@ def tile_selfprojectiondev_pa_t_kernel(tc, x, o_xj, p_xj, rel_o_xj, out_0, out_1
                 transposes(s + 1)
                 if s % 2 == 0 and (s + 1) // 2 + XRING < NB // 2:
                     load_pair((s + 1) // 2 + XRING, False)
-            g = due(s, 12, NG)
-            if g is not None:
-                stats2_out(g, g + 3, 16)
-            g = due(s, 11, NG)
-            if g is not None:
-                stats2_sum(g)
+            if g1 is not None:
+                stats1_matmul(g1)
+            for bl in range(4):
+                g = due(s, 6 + bl, NG)
+                if g is not None:
+                    standardise(g, bl)
+            if kp is not None:
+                var_step(kp, 2)
+                root(kp)
             g = due(s, 10, NG)
-            if g is not None:
-                tanh_u(g)
-            g = due(s, 9, NG)
             if g is not None:
                 quantise_t(g)
                 matmul_u(g)
-            k = due(s, 5, NG + 3)
-            if k is not None:
-                recip(k, 0 if k < NG else 16, 20 if k >= 3 else 16)
-                if k >= 3:
-                    finish(k - 3, k, 16)
-            for bl in range(4):
-                g = due(s, 5 + bl, NG)
-                if g is not None:
-                    standardise(g, bl)
-            k = due(s, 1, NG + 3)
-            if k is not None:
-                if k < NG:
-                    stats1_out(k)
-                chain(k, 0 if k < NG else 16, 20 if k >= 3 else 16)
-            g = due(s, 0, NG)
+            if kf is not None and kf >= 3:
+                finish(kf - 3, kf, 16)
+            g = due(s, 11, NG)
             if g is not None:
-                stats1_sum(g)
+                tanh_u(g)
+            g = due(s, 12, NG)
+            if g is not None:
+                stats2_sum(g)
             if rb == NB:
                 softmax_finish()

@@ -22,9 +22,10 @@ EPS = 1e-5
 FLOPS = 2 * NB * ND * (2 * NI * NJ * NP + NP * NI * NP)
 
 PIN = True
-LAG = 6
-FIRST = 5
+LAG = 4
+FIRST = 6
 DUP = 2
+KL = 4
 XRING = 10
 NG = NB // 4
 
@@ -60,8 +61,9 @@ def tile_selfprojectiondev_pa_t_kernel(tc, x, o_xj, p_xj, rel_o_xj, out_0, out_1
         nc.vector.memset(bd1024[:], 0.0)
         for q in range(4):
             nc.vector.memset(bd1024[32 * q : 32 * q + 32, 32 * q : 32 * q + 32], 1.0 / 1024.0)
-        half = const.tile([P, 24], F32, name="half")
+        half = const.tile([P, 32], F32, name="half")
         nc.vector.memset(half[:], 0.5)
+        scratch = const.tile([P, 1], F32, name="scratch")
         negmax = const.tile([P, P], F32, name="negmax")
         nc.vector.memset(negmax[:], 0.0)
         expsum = const.tile([P, P], F32, name="expsum")
@@ -246,9 +248,9 @@ def tile_selfprojectiondev_pa_t_kernel(tc, x, o_xj, p_xj, rel_o_xj, out_0, out_1
 
         def chain_tiles(key):
             if key not in me:
-                me[key] = mepool.tile([P, 2, 24], F32, name="me", tag="me")
-                wk[key] = mepool.tile([P, 5, 24], F32, name="wk", tag="wk")
-                rs[key] = mepool.tile([P, 24], F32, name="rs", tag="rs")
+                me[key] = mepool.tile([P, 2, 32], F32, name="me", tag="me")
+                wk[key] = mepool.tile([P, 5, 32], F32, name="wk", tag="wk")
+                rs[key] = mepool.tile([P, 32], F32, name="rs", tag="rs")
 
         sqms = {}
 
@@ -256,7 +258,7 @@ def tile_selfprojectiondev_pa_t_kernel(tc, x, o_xj, p_xj, rel_o_xj, out_0, out_1
             sv = st[g][:].rearrange("p k (h s) -> p k h s", s=3)
             sqm = mepool.tile([P, 16, 2], F32, name="sqm", tag="sqm")
             sqms[g] = sqm
-            nc.scalar.activation(out=sqm[:], in_=sv[:, :, :, 1], func=ACT.Square)
+            nc.vector.tensor_tensor(out=sqm[:], in0=sv[:, :, :, 1], in1=sv[:, :, :, 1], op=ALU.mult)
 
         def stats1_matmul(g):
             sv = st[g][:].rearrange("p k (h s) -> p k h s", s=3)
@@ -271,7 +273,9 @@ def tile_selfprojectiondev_pa_t_kernel(tc, x, o_xj, p_xj, rel_o_xj, out_0, out_1
             nc.vector.tensor_reduce(out=me[g][:, :, 0:16], in_=stp[g][:], axis=AX.X, op=ALU.add)
 
         def cols(k):
-            return (0 if k < NG else 16), (20 if k >= 3 else 16)
+            if k == NG:
+                return 16, 32
+            return 0, (20 if k >= KL else 16)
 
         def var_step(k, i):
             c0, c1 = cols(k)
@@ -283,23 +287,29 @@ def tile_selfprojectiondev_pa_t_kernel(tc, x, o_xj, p_xj, rel_o_xj, out_0, out_1
             else:
                 nc.vector.tensor_tensor(out=w[:, 2, c0:c1], in0=w[:, 1, c0:c1], in1=w[:, 0, c0:c1], op=ALU.subtract)
 
+        F_Z = 16384.0 / 16383.0
+        F_U = 1024.0 / 1023.0
+
+        def warm(func):
+            nc.scalar.activation(out=scratch[:], in_=half[:, 0:1], func=func)
+
         def root(k):
             c0, c1 = cols(k)
             w = wk[k]
-            nc.gpsimd.tensor_tensor(out=w[:, 3, c0:c1], in0=w[:, 2, c0:c1], in1=half[:, c0:c1], op=ALU.pow)
+            if k < NG - 1:
+                nc.gpsimd.tensor_tensor(out=w[:, 3, c0:c1], in0=w[:, 2, c0:c1], in1=half[:, c0:c1], op=ALU.pow)
+            else:
+                if c0 < 16:
+                    nc.scalar.activation(out=w[:, 3, c0:16], in_=w[:, 2, c0:16], func=ACT.Sqrt, scale=F_Z)
+                nc.scalar.activation(out=w[:, 3, 16:c1], in_=w[:, 2, 16:c1], func=ACT.Sqrt, scale=F_U)
+                nc.scalar.activation(out=w[:, 4, c0:c1], in_=w[:, 3, c0:c1], func=ACT.Copy, scale=1.0, bias=EPS)
 
         def scale_std(k):
+            c0, c1 = cols(k)
             w = wk[k]
-            if k < NG:
-                nc.scalar.activation(
-                    out=w[:, 4, 0:16], in_=w[:, 3, 0:16], func=ACT.Copy,
-                    scale=(16384.0 / 16383.0) ** 0.5, bias=EPS,
-                )
-            if k >= 3:
-                nc.scalar.activation(
-                    out=w[:, 4, 16:20], in_=w[:, 3, 16:20], func=ACT.Copy,
-                    scale=(1024.0 / 1023.0) ** 0.5, bias=EPS,
-                )
+            nc.scalar.activation(out=w[:, 4, 0:16], in_=w[:, 3, 0:16], func=ACT.Copy, scale=F_Z ** 0.5, bias=EPS)
+            if c1 > 16:
+                nc.scalar.activation(out=w[:, 4, 16:c1], in_=w[:, 3, 16:c1], func=ACT.Copy, scale=F_U ** 0.5, bias=EPS)
 
         def recip(k):
             c0, c1 = cols(k)
@@ -357,14 +367,21 @@ def tile_selfprojectiondev_pa_t_kernel(tc, x, o_xj, p_xj, rel_o_xj, out_0, out_1
             stp[("u", g)] = ps
             nc.tensor.matmul(ps[:], lhsT=bd1024[:], rhs=s[:], start=True, stop=True)
 
-        def stats2_out(g, key, c0):
+        def u_place(g):
+            if g + KL < NG:
+                return g + KL, 16
+            return NG, 16 + 4 * (g + KL - NG)
+
+        def stats2_out(g):
+            key, c0 = u_place(g)
             chain_tiles(key)
             nc.scalar.copy(
                 out=me[key][:, :, c0 : c0 + 4],
                 in_=stp[("u", g)][:].rearrange("p (k d) -> p k d", k=2),
             )
 
-        def finish(g, key, c0):
+        def finish(g):
+            key, c0 = u_place(g)
             ov = vpool.tile([P, ND, NP], F32, name="ov", tag="ov")
             for d in range(ND):
                 nc.vector.tensor_scalar(
@@ -412,65 +429,78 @@ def tile_selfprojectiondev_pa_t_kernel(tc, x, o_xj, p_xj, rel_o_xj, out_0, out_1
             return g if rem == 0 and 0 <= g < count else None
 
         transposes(0)
-        for s in range(FIRST + 4 * (NG + 2) + 7):
+        for s in range(FIRST + 4 * (NG - 1) + 16):
             rb = s - LAG
-            kp = due(s, 2, NG + 3)
-            kf = due(s, 6, NG + 3)
-            g1 = due(s, 1, NG)
-            if kf is not None:
+            kp = due(s, 2, NG)
+            kf = due(s, 6, NG)
+            g0 = due(s, 0, NG)
+            if kf is not None and kf < NG - 1:
                 scale_std(kf)
-            if 0 <= s - 2 < NB:
-                tanh_z(s - 2)
-            if g1 is not None:
-                square_means(g1)
-            g = due(s, 13, NG)
-            if g is not None:
-                stats2_out(g, g + 3, 16)
             if s < NB:
                 evacuate(s)
-            if 0 <= rb < NB:
-                row_max(rb)
-                row_exp(rb)
-            if kp is not None and kp < NG:
-                stats1_out(kp)
-            if kf is not None:
-                recip(kf)
+            if 0 <= s - 2 < NB:
+                tanh_z(s - 2)
+            g = due(s, 15, NG)
+            if g is not None:
+                stats2_out(g)
             if 0 <= s - 1 < NB:
                 quantise_x(s - 1)
             if kp is not None:
                 var_step(kp, 0)
-            if 0 <= s - 2 < NB:
-                stats_z(s - 2)
+            if 0 <= s - 3 < NB:
+                stats_z(s - 3)
+            if g0 is not None:
+                square_means(g0)
             if kp is not None:
                 var_step(kp, 1)
+            if 0 <= rb < NB:
+                row_max(rb)
+                row_exp(rb)
+            if kp is not None:
+                var_step(kp, 2)
+                if kp == NG - 1:
+                    warm(ACT.Sqrt)
+                root(kp)
+                if kp == NG - 1:
+                    warm(ACT.Tanh)
+            if kf is not None:
+                recip(kf)
             if 0 <= rb + 1 < NB:
                 matmul_r(rb + 1)
-            if 0 <= s - 1 < NB:
-                matmul_z(s - 1)
             if s + 1 < NB:
                 transposes(s + 1)
                 if s % 2 == 0 and (s + 1) // 2 + XRING < NB // 2:
                     load_pair((s + 1) // 2 + XRING, False)
-            if g1 is not None:
-                stats1_matmul(g1)
-            for bl in range(4):
-                g = due(s, 6 + bl, NG)
-                if g is not None:
-                    standardise(g, bl)
-            if kp is not None:
-                var_step(kp, 2)
-                root(kp)
+            if 0 <= s - 1 < NB:
+                matmul_z(s - 1)
+            if g0 is not None:
+                stats1_matmul(g0)
             g = due(s, 10, NG)
             if g is not None:
                 quantise_t(g)
                 matmul_u(g)
-            if kf is not None and kf >= 3:
-                finish(kf - 3, kf, 16)
-            g = due(s, 11, NG)
-            if g is not None:
-                tanh_u(g)
+            for bl in range(4):
+                g = due(s, 6 + bl, NG)
+                if g is not None:
+                    standardise(g, bl)
+            if kf is not None and kf >= KL:
+                finish(kf - KL)
             g = due(s, 12, NG)
             if g is not None:
+                tanh_u(g)
+                if g == NG - 1:
+                    warm(ACT.Sqrt)
+            g = due(s, 14, NG)
+            if g is not None:
                 stats2_sum(g)
-            if rb == NB:
+            g = due(s, 1, NG)
+            if g is not None:
+                stats1_out(g)
+            if s == FIRST + 4 * (NG - 1) + 10:
                 softmax_finish()
+        for i in range(3):
+            var_step(NG, i)
+        root(NG)
+        recip(NG)
+        for g in range(NG - 1, NG - KL - 1, -1):
+            finish(g)

@@ -24,7 +24,7 @@ FLOPS = 2 * NB * ND * (2 * NI * NJ * NP + NP * NI * NP)
 PIN = True
 LAG = 4
 FIRST = 6
-DUP = 2
+DUP = 1
 KL = 4
 XRING = 10
 NG = NB // 4

@@ -55,12 +55,17 @@ def tile_selfprojectiondev_pa_t_kernel(tc, x, o_xj, p_xj, rel_o_xj, out_0, out_1
         make_identity(nc, ident[:])
         ones256 = const.tile([P, P], F32, name="ones256")
         nc.vector.memset(ones256[:], 1.0 / 256.0)
+        negones256 = const.tile([P, P], F32, name="negones256")
+        nc.vector.memset(negones256[:], -1.0 / 256.0)
         ones16k = const.tile([P, P], F32, name="ones16k")
         nc.vector.memset(ones16k[:], 1.0 / 16384.0)
         bd1024 = const.tile([P, P], F32, name="bd1024")
         nc.vector.memset(bd1024[:], 0.0)
+        negbd1024 = const.tile([P, P], F32, name="negbd1024")
+        nc.vector.memset(negbd1024[:], 0.0)
         for q in range(4):
             nc.vector.memset(bd1024[32 * q : 32 * q + 32, 32 * q : 32 * q + 32], 1.0 / 1024.0)
+            nc.vector.memset(negbd1024[32 * q : 32 * q + 32, 32 * q : 32 * q + 32], -1.0 / 1024.0)
         half = const.tile([P, 32], F32, name="half")
         nc.vector.memset(half[:], 0.5)
         scratch = const.tile([P, 1], F32, name="scratch")
@@ -264,7 +269,7 @@ def tile_selfprojectiondev_pa_t_kernel(tc, x, o_xj, p_xj, rel_o_xj, out_0, out_1
             sv = st[g][:].rearrange("p k (h s) -> p k h s", s=3)
             ps = ps_st.tile([P, 2, 16, 2], F32, name="stps", tag="stps")
             stp[g] = ps
-            nc.tensor.matmul(ps[:, 0], lhsT=ones256[:], rhs=sv[:, :, :, 1], start=True, stop=True)
+            nc.tensor.matmul(ps[:, 0], lhsT=negones256[:], rhs=sv[:, :, :, 1], start=True, stop=True)
             nc.tensor.matmul(ps[:, 1], lhsT=ones16k[:], rhs=sv[:, :, :, 2], start=True, stop=False)
             nc.tensor.matmul(ps[:, 1], lhsT=ones256[:], rhs=sqms[g][:], start=False, stop=True)
 
@@ -318,14 +323,15 @@ def tile_selfprojectiondev_pa_t_kernel(tc, x, o_xj, p_xj, rel_o_xj, out_0, out_1
         def standardise(g, bl):
             if bl == 0:
                 tg[g] = tgpool.tile([P, 2048], BF16, name="tg", tag="tg", align_bytes=64)
+            eng = nc.gpsimd if (bl == 0 and g < NG - 1) else nc.vector
             for d in range(ND):
                 col = bl * 4 + d
-                nc.vector.tensor_scalar(
+                eng.tensor_scalar(
                     out=tg[g][:, (d * 4 + bl) * P : (d * 4 + bl + 1) * P],
                     in0=th[g][:, bl, d * P : (d + 1) * P],
                     scalar1=me[g][:, 0, col : col + 1],
                     scalar2=rs[g][:, col : col + 1],
-                    op0=ALU.subtract,
+                    op0=ALU.add,
                     op1=ALU.mult,
                 )
 
@@ -365,7 +371,8 @@ def tile_selfprojectiondev_pa_t_kernel(tc, x, o_xj, p_xj, rel_o_xj, out_0, out_1
             )
             ps = ps_st.tile([P, 8], F32, name="stps2", tag="stps")
             stp[("u", g)] = ps
-            nc.tensor.matmul(ps[:], lhsT=bd1024[:], rhs=s[:], start=True, stop=True)
+            nc.tensor.matmul(ps[:, 0:4], lhsT=negbd1024[:], rhs=s[:, 0:4], start=True, stop=True)
+            nc.tensor.matmul(ps[:, 4:8], lhsT=bd1024[:], rhs=s[:, 4:8], start=True, stop=True)
 
         def u_place(g):
             if g + KL < NG:
@@ -383,13 +390,14 @@ def tile_selfprojectiondev_pa_t_kernel(tc, x, o_xj, p_xj, rel_o_xj, out_0, out_1
         def finish(g):
             key, c0 = u_place(g)
             ov = vpool.tile([P, ND, NP], F32, name="ov", tag="ov")
+            eng = nc.gpsimd if key < NG else nc.vector
             for d in range(ND):
-                nc.vector.tensor_scalar(
+                eng.tensor_scalar(
                     out=ov[:, d, :],
                     in0=vv[g][:, 0, d, :],
                     scalar1=me[key][:, 0, c0 + d : c0 + d + 1],
                     scalar2=rs[key][:, c0 + d : c0 + d + 1],
-                    op0=ALU.subtract,
+                    op0=ALU.add,
                     op1=ALU.mult,
                 )
             for bl in range(4):
@@ -398,12 +406,16 @@ def tile_selfprojectiondev_pa_t_kernel(tc, x, o_xj, p_xj, rel_o_xj, out_0, out_1
                     in_=ov[32 * bl : 32 * bl + 32, :, :],
                 )
 
-        def softmax_finish():
+        sm = {}
+
+        def softmax_a():
             tp = ps_xt.tile([P, 2, P], F32, name="smps", tag="xtb")
+            sm["tp"] = tp
             nc.tensor.transpose(tp[:, 0, :], negmax[:], ident[:])
             nc.tensor.transpose(tp[:, 1, :], expsum[:], ident[:])
-            nmt = tp[0:NB, 0, :].rearrange("b (d n) -> b d n", d=ND)
-            smt = tp[0:NB, 1, :].rearrange("b (d n) -> b d n", d=ND)
+
+        def softmax_b():
+            nmt = sm["tp"][0:NB, 0, :].rearrange("b (d n) -> b d n", d=ND)
             gmin = const.tile([NB, ND], F32, name="gmin")
             nc.vector.tensor_reduce(out=gmin[:], in_=nmt, axis=AX.X, op=ALU.min)
             diff = const.tile([NB, ND, NP], F32, name="diff")
@@ -411,9 +423,13 @@ def tile_selfprojectiondev_pa_t_kernel(tc, x, o_xj, p_xj, rel_o_xj, out_0, out_1
                 out=diff[:], in0=gmin[:].unsqueeze(2).to_broadcast([NB, ND, NP]), in1=nmt, op=ALU.subtract
             )
             ex = const.tile([NB, ND, NP], F32, name="ex")
+            sm["ex"] = ex
             nc.scalar.activation(out=ex[:], in_=diff[:], func=ACT.Exp)
+
+        def softmax_c():
+            smt = sm["tp"][0:NB, 1, :].rearrange("b (d n) -> b d n", d=ND)
             wgt = const.tile([NB, ND, NP], F32, name="wgt")
-            nc.vector.tensor_tensor(out=wgt[:], in0=ex[:], in1=smt, op=ALU.mult)
+            nc.vector.tensor_tensor(out=wgt[:], in0=sm["ex"][:], in1=smt, op=ALU.mult)
             tot = const.tile([NB, ND], F32, name="tot")
             nc.vector.tensor_reduce(out=tot[:], in_=wgt[:], axis=AX.X, op=ALU.add)
             rtot = const.tile([NB, ND], F32, name="rtot")
@@ -496,8 +512,12 @@ def tile_selfprojectiondev_pa_t_kernel(tc, x, o_xj, p_xj, rel_o_xj, out_0, out_1
             g = due(s, 1, NG)
             if g is not None:
                 stats1_out(g)
+            if s == FIRST + 4 * (NG - 1) + 3:
+                softmax_a()
             if s == FIRST + 4 * (NG - 1) + 10:
-                softmax_finish()
+                softmax_b()
+            if s == FIRST + 4 * (NG - 1) + 11:
+                softmax_c()
         for i in range(3):
             var_step(NG, i)
         root(NG)

@@ -53,10 +53,10 @@ def tile_selfprojectiondev_pa_t_kernel(tc, x, o_xj, p_xj, rel_o_xj, out_0, out_1
 
         ident = const.tile([P, P], F32, name="ident")
         make_identity(nc, ident[:])
-        ones256 = const.tile([P, P], F32, name="ones256")
-        nc.vector.memset(ones256[:], 1.0 / 256.0)
-        negones256 = const.tile([P, P], F32, name="negones256")
-        nc.vector.memset(negones256[:], -1.0 / 256.0)
+        ones128 = const.tile([P, P], F32, name="ones128")
+        nc.vector.memset(ones128[:], 1.0 / 128.0)
+        negones128 = const.tile([P, P], F32, name="negones128")
+        nc.vector.memset(negones128[:], -1.0 / 128.0)
         ones16k = const.tile([P, P], F32, name="ones16k")
         nc.vector.memset(ones16k[:], 1.0 / 16384.0)
         bd1024 = const.tile([P, P], F32, name="bd1024")
@@ -76,59 +76,59 @@ def tile_selfprojectiondev_pa_t_kernel(tc, x, o_xj, p_xj, rel_o_xj, out_0, out_1
 
         xs = {}
 
-        def load_pair(k, split):
+        def load_pair(k):
             t = xpool.tile([P, 2, 4, NJ], BF16, name="xs", tag="xs")
             xs[k] = t
-            if split:
-                for bi in range(2):
-                    nc.sync.dma_start(
-                        out=t[:, bi].rearrange("q c j -> q (c j)"),
-                        in_=x[2 * k + bi].rearrange("(q c) j -> q (c j)", c=4),
-                    )
-            else:
-                nc.sync.dma_start(
-                    out=t[:].rearrange("q b c j -> q b (c j)"),
-                    in_=x[2 * k : 2 * k + 2].rearrange("b (q c) j -> q b (c j)", c=4),
-                )
-
-        load_pair(0, True)
+            nc.sync.dma_start(
+                out=t[:].rearrange("q b c j -> q b (c j)"),
+                in_=x[2 * k : 2 * k + 2].rearrange("b (q c) j -> q b (c j)", c=4),
+            )
 
         wraw = const.tile([P, 3, ND, 4, NP], BF16, name="wraw")
-        for kind, w in ((0, o_xj), (1, rel_o_xj)):
+
+        def load_weights(kind, w):
             wv = w.rearrange("d (u p e) n -> u p d (e n)", u=2, p=P, e=2)
             for u in range(2):
-                nc.scalar.dma_start(
+                nc.sync.dma_start(
                     out=wraw[:, kind, :, 2 * u : 2 * u + 2, :].rearrange("p d e n -> p d (e n)"),
                     in_=wv[u],
                 )
-        nc.scalar.dma_start(
+
+        first = xpool.tile([P, 2, 4, NJ], BF16, name="xs", tag="xs")
+        xs[0] = first
+
+        def load_item(bi):
+            nc.sync.dma_start(
+                out=first[:, bi].rearrange("q c j -> q (c j)"),
+                in_=x[bi].rearrange("(q c) j -> q (c j)", c=4),
+            )
+
+        load_item(0)
+        load_weights(0, o_xj)
+        load_item(1)
+        load_weights(1, rel_o_xj)
+        nc.sync.dma_start(
             out=wraw[:, 2].rearrange("q d c n -> q d (c n)"),
             in_=p_xj.rearrange("d (q c) n -> q d (c n)", c=4),
         )
         for k in range(1, XRING):
-            load_pair(k, False)
+            load_pair(k)
 
         wgrp = const.tile([P, 3, P, 4], BF16, name="wgrp", align_bytes=64)
         wcod = const.tile([P, 3 * P], U32, name="wcod", align_bytes=64)
         wsc = const.tile([P, 3 * P], U8, name="wsc", align_bytes=64)
-        nc.vector.tensor_copy(
-            out=wgrp[:, 0:2].rearrange("p k (d n) t -> p (k d) n t", d=ND),
-            in_=wraw[:, 0:2].rearrange("p k d t n -> p (k d) n t"),
-        )
-        nc.vector.tensor_copy(
-            out=wgrp[:, 2].rearrange("p (d n) t -> p d n t", d=ND),
-            in_=wraw[:, 2].rearrange("p d t n -> p d n t"),
-        )
-        nc.vector.quantize_mx(
-            out=wcod[:, 0 : 2 * P].bitcast(FP8X4),
-            scales=wsc[:, 0 : 2 * P],
-            in_=wgrp[:, 0:2].rearrange("p k w t -> p (k w t)"),
-        )
-        nc.vector.quantize_mx(
-            out=wcod[:, 2 * P : 3 * P].bitcast(FP8X4),
-            scales=wsc[:, 2 * P : 3 * P],
-            in_=wgrp[:, 2].rearrange("p w t -> p (w t)"),
-        )
+
+        def quantise_weights(kind):
+            nc.vector.tensor_copy(
+                out=wgrp[:, kind].rearrange("p (d n) t -> p d n t", d=ND),
+                in_=wraw[:, kind].rearrange("p d t n -> p d n t"),
+            )
+            nc.vector.quantize_mx(
+                out=wcod[:, kind * P : (kind + 1) * P].bitcast(FP8X4),
+                scales=wsc[:, kind * P : (kind + 1) * P],
+                in_=wgrp[:, kind].rearrange("p w t -> p (w t)"),
+            )
+
 
         def wslice(kind):
             return (
@@ -235,10 +235,11 @@ def tile_selfprojectiondev_pa_t_kernel(tc, x, o_xj, p_xj, rel_o_xj, out_0, out_1
         def stats_z(b):
             g, bl = b // 4, b % 4
             if bl == 0:
-                st[g] = stpool.tile([P, 16, 6], F32, name="st", tag="st")
-            for d in range(ND):
+                st[g] = stpool.tile([P, 8, 6], F32, name="st", tag="st")
+            for pair in range(ND // 2):
                 nc.vector.bn_stats(
-                    out=st[g][:, bl * 4 + d, :], in_=th[g][:, bl, d * P : (d + 1) * P]
+                    out=st[g][:, bl * 2 + pair, :],
+                    in_=th[g][:, bl, pair * 256 : (pair + 1) * 256].rearrange("p (e w) -> p w e", e=2),
                 )
 
         me = {}
@@ -261,21 +262,23 @@ def tile_selfprojectiondev_pa_t_kernel(tc, x, o_xj, p_xj, rel_o_xj, out_0, out_1
 
         def square_means(g):
             sv = st[g][:].rearrange("p k (h s) -> p k h s", s=3)
-            sqm = mepool.tile([P, 16, 2], F32, name="sqm", tag="sqm")
+            sqm = mepool.tile([P, 8, 2], F32, name="sqm", tag="sqm")
             sqms[g] = sqm
             nc.vector.tensor_tensor(out=sqm[:], in0=sv[:, :, :, 1], in1=sv[:, :, :, 1], op=ALU.mult)
 
         def stats1_matmul(g):
             sv = st[g][:].rearrange("p k (h s) -> p k h s", s=3)
-            ps = ps_st.tile([P, 2, 16, 2], F32, name="stps", tag="stps")
+            ps = ps_st.tile([P, 2, 8, 2], F32, name="stps", tag="stps")
             stp[g] = ps
-            nc.tensor.matmul(ps[:, 0], lhsT=negones256[:], rhs=sv[:, :, :, 1], start=True, stop=True)
+            nc.tensor.matmul(ps[:, 0], lhsT=negones128[:], rhs=sv[:, :, :, 1], start=True, stop=True)
             nc.tensor.matmul(ps[:, 1], lhsT=ones16k[:], rhs=sv[:, :, :, 2], start=True, stop=False)
-            nc.tensor.matmul(ps[:, 1], lhsT=ones256[:], rhs=sqms[g][:], start=False, stop=True)
+            nc.tensor.matmul(ps[:, 1], lhsT=ones128[:], rhs=sqms[g][:], start=False, stop=True)
 
         def stats1_out(g):
             chain_tiles(g)
-            nc.vector.tensor_reduce(out=me[g][:, :, 0:16], in_=stp[g][:], axis=AX.X, op=ALU.add)
+            nc.vector.tensor_copy(
+                out=me[g][:, :, 0:16], in_=stp[g][:].rearrange("p k h s -> p k (h s)")
+            )
 
         def cols(k):
             if k == NG:
@@ -459,6 +462,8 @@ def tile_selfprojectiondev_pa_t_kernel(tc, x, o_xj, p_xj, rel_o_xj, out_0, out_1
             g = due(s, 15, NG)
             if g is not None:
                 stats2_out(g)
+            if s < 3:
+                quantise_weights(s)
             if 0 <= s - 1 < NB:
                 quantise_x(s - 1)
             if kp is not None:
@@ -486,7 +491,7 @@ def tile_selfprojectiondev_pa_t_kernel(tc, x, o_xj, p_xj, rel_o_xj, out_0, out_1
             if s + 1 < NB:
                 transposes(s + 1)
                 if s % 2 == 0 and (s + 1) // 2 + XRING < NB // 2:
-                    load_pair((s + 1) // 2 + XRING, False)
+                    load_pair((s + 1) // 2 + XRING)
             if 0 <= s - 1 < NB:
                 matmul_z(s - 1)
             if g0 is not None:

@@ -326,10 +326,9 @@ def tile_selfprojectiondev_pa_t_kernel(tc, x, o_xj, p_xj, rel_o_xj, out_0, out_1
         def standardise(g, bl):
             if bl == 0:
                 tg[g] = tgpool.tile([P, 2048], BF16, name="tg", tag="tg", align_bytes=64)
-            eng = nc.gpsimd if (bl == 0 and g < NG - 1) else nc.vector
             for d in range(ND):
                 col = bl * 4 + d
-                eng.tensor_scalar(
+                nc.vector.tensor_scalar(
                     out=tg[g][:, (d * 4 + bl) * P : (d * 4 + bl + 1) * P],
                     in0=th[g][:, bl, d * P : (d + 1) * P],
                     scalar1=me[g][:, 0, col : col + 1],

@@ -20,14 +20,29 @@ NP = 32
 P = 128
 EPS = 1e-5
 FLOPS = 2 * NB * ND * (2 * NI * NJ * NP + NP * NI * NP)
+F_Z = (NI * NP) / (NI * NP - 1.0)
+F_U = (NP * NP) / (NP * NP - 1.0)
 
-PIN = True
-LAG = 4
-FIRST = 6
-DUP = 1
-KL = 4
-XRING = 10
 NG = NB // 4
+XRING = 5
+
+T_AHEAD = 2
+XT = 5
+ZB = 2
+V_MOD, V_SET = 2, (1,)
+CHUNK = 4
+ROOT_S = True
+PW = 16
+LEAD = 2
+R_AHEAD = 4
+GS = 3
+MAX_AT = (34, 35)
+STD_V, STD_S = 9, 7
+ORDER16 = "vsvsvvsvsvvsvsvs"
+UCH = ((0, 8, 27),)
+U_S = True
+FIN = ("v", "v", "s", "v", "g", "v", "s", "v")
+INV, INV_AT = 5, 18
 
 
 def tile_selfprojectiondev_pa_t_kernel(tc, x, o_xj, p_xj, rel_o_xj, out_0, out_1):
@@ -36,105 +51,105 @@ def tile_selfprojectiondev_pa_t_kernel(tc, x, o_xj, p_xj, rel_o_xj, out_0, out_1
         const = ctx.enter_context(tc.tile_pool(name="const", bufs=1))
         xpool = ctx.enter_context(tc.tile_pool(name="xpool", bufs=XRING))
         gpool = ctx.enter_context(tc.tile_pool(name="gpool", bufs=3))
-        cpool = ctx.enter_context(tc.tile_pool(name="cpool", bufs=LAG + 1))
-        thpool = ctx.enter_context(tc.tile_pool(name="thpool", bufs=4))
-        stpool = ctx.enter_context(tc.tile_pool(name="stpool", bufs=2))
-        mepool = ctx.enter_context(tc.tile_pool(name="mepool", bufs=5))
+        cpool = ctx.enter_context(tc.tile_pool(name="cpool", bufs=NB))
+        thpool = ctx.enter_context(tc.tile_pool(name="thpool", bufs=NG))
+        smpool = ctx.enter_context(tc.tile_pool(name="smpool", bufs=8))
         tgpool = ctx.enter_context(tc.tile_pool(name="tgpool", bufs=2))
-        vpool = ctx.enter_context(tc.tile_pool(name="vpool", bufs=5))
+        vpool = ctx.enter_context(tc.tile_pool(name="vpool", bufs=NG))
         jpool = ctx.enter_context(tc.tile_pool(name="jpool", bufs=2))
-        ps_xt = ctx.enter_context(tc.psum_pool(name="ps_xt", bufs=3))
-        ps_z = ctx.enter_context(tc.psum_pool(name="ps_z", bufs=1))
-        ps_r = ctx.enter_context(tc.psum_pool(name="ps_r", bufs=2))
-        ps_st = ctx.enter_context(tc.psum_pool(name="ps_st", bufs=1))
-        ps_u = ctx.enter_context(tc.psum_pool(name="ps_u", bufs=1))
-        if PIN:
-            ctx.enter_context(tc.manual_schedule())
+        ps_xt = ctx.enter_context(tc.psum_pool(name="ps_xt", bufs=XT))
+        ps_z = ctx.enter_context(tc.psum_pool(name="ps_z", bufs=ZB))
+        ps_s = ctx.enter_context(tc.psum_pool(name="ps_s", bufs=8 - XT - ZB))
+        ctx.enter_context(tc.manual_schedule())
 
-        ident = const.tile([P, P], F32, name="ident")
-        make_identity(nc, ident[:])
-        ones128 = const.tile([P, P], F32, name="ones128")
-        nc.vector.memset(ones128[:], 1.0 / 128.0)
-        negones128 = const.tile([P, P], F32, name="negones128")
-        nc.vector.memset(negones128[:], -1.0 / 128.0)
-        ones16k = const.tile([P, P], F32, name="ones16k")
-        nc.vector.memset(ones16k[:], 1.0 / 16384.0)
-        bd1024 = const.tile([P, P], F32, name="bd1024")
-        nc.vector.memset(bd1024[:], 0.0)
-        negbd1024 = const.tile([P, P], F32, name="negbd1024")
-        nc.vector.memset(negbd1024[:], 0.0)
-        for q in range(4):
-            nc.vector.memset(bd1024[32 * q : 32 * q + 32, 32 * q : 32 * q + 32], 1.0 / 1024.0)
-            nc.vector.memset(negbd1024[32 * q : 32 * q + 32, 32 * q : 32 * q + 32], -1.0 / 1024.0)
+        xs = {}
+
+        def x_tile(k):
+            xs[k] = xpool.tile([P, 2, 4, NJ], BF16, name="xs", tag="xs")
+
+        def load_half_item(k, bi, h):
+            nc.sync.dma_start(
+                out=xs[k][:, bi, 2 * h : 2 * h + 2].rearrange("q c j -> q (c j)"),
+                in_=x[2 * k + bi].rearrange("(q h c) j -> h q (c j)", h=2, c=2)[h],
+            )
+
+        def load_item(k, bi):
+            nc.sync.dma_start(
+                out=xs[k][:, bi].rearrange("q c j -> q (c j)"),
+                in_=x[2 * k + bi].rearrange("(q c) j -> q (c j)", c=4),
+            )
+
+        def load_pair(k):
+            x_tile(k)
+            nc.sync.dma_start(
+                out=xs[k][:].rearrange("q b c j -> q b (c j)"),
+                in_=x[2 * k : 2 * k + 2].rearrange("b (q c) j -> q b (c j)", c=4),
+            )
+
+        wraw = [const.tile([P, ND, 4, NP], BF16, name="wraw%d" % k) for k in range(3)]
+
+        def load_w(kind, w):
+            wv = w.rearrange("d (u p e) n -> u p d (e n)", u=2, p=P, e=2)
+            for u in range(2):
+                nc.sync.dma_start(
+                    out=wraw[kind][:, :, 2 * u : 2 * u + 2, :].rearrange("p d e n -> p d (e n)"),
+                    in_=wv[u],
+                )
+
+        x_tile(0)
+        load_half_item(0, 0, 0)
+        load_half_item(0, 0, 1)
+        load_w(0, o_xj)
+        load_item(0, 1)
+        x_tile(1)
+        load_item(1, 0)
+        load_item(1, 1)
+        load_pair(2)
+        load_w(1, rel_o_xj)
+        nc.sync.dma_start(
+            out=wraw[2][:].rearrange("q d c n -> q d (c n)"),
+            in_=p_xj.rearrange("d (q c) n -> q d (c n)", c=4),
+        )
+        for k in range(3, XRING):
+            load_pair(k)
+
         half = const.tile([P, 32], F32, name="half")
         nc.vector.memset(half[:], 0.5)
         scratch = const.tile([P, 1], F32, name="scratch")
+        nc.scalar.activation(out=scratch[:], in_=half[:, 0:1], func=ACT.Tanh)
+        ident = const.tile([P, P], F32, name="ident")
+        make_identity(nc, ident[:])
+        wz = const.tile([P, P], F32, name="wz")
+        nc.vector.memset(wz[:], 1.0 / 16384.0)
+        wu = const.tile([P, P], F32, name="wu")
+        nc.vector.memset(wu[:], 0.0)
+        for q in range(4):
+            block = slice(32 * q, 32 * q + 32)
+            nc.vector.memset(wu[block, block], 1.0 / 1024.0)
         negmax = const.tile([P, P], F32, name="negmax")
         nc.vector.memset(negmax[:], 0.0)
         expsum = const.tile([P, P], F32, name="expsum")
         nc.vector.memset(expsum[:], 0.0)
 
-        xs = {}
+        stz = const.tile([P, NB * 2, 6], F32, name="stz")
+        stu = const.tile([P, NG * 2, 6], F32, name="stu")
+        nz, nu = NB * ND, NG * ND
+        sz = const.tile([P, 7, nz], F32, name="sz")
+        su = const.tile([P, 7, nu], F32, name="su")
+        wq = {}
 
-        def load_pair(k):
-            t = xpool.tile([P, 2, 4, NJ], BF16, name="xs", tag="xs")
-            xs[k] = t
-            nc.sync.dma_start(
-                out=t[:].rearrange("q b c j -> q b (c j)"),
-                in_=x[2 * k : 2 * k + 2].rearrange("b (q c) j -> q b (c j)", c=4),
-            )
-
-        wraw = const.tile([P, 3, ND, 4, NP], BF16, name="wraw")
-
-        def load_weights(kind, w):
-            wv = w.rearrange("d (u p e) n -> u p d (e n)", u=2, p=P, e=2)
-            for u in range(2):
-                nc.sync.dma_start(
-                    out=wraw[:, kind, :, 2 * u : 2 * u + 2, :].rearrange("p d e n -> p d (e n)"),
-                    in_=wv[u],
-                )
-
-        first = xpool.tile([P, 2, 4, NJ], BF16, name="xs", tag="xs")
-        xs[0] = first
-
-        def load_item(bi):
-            nc.sync.dma_start(
-                out=first[:, bi].rearrange("q c j -> q (c j)"),
-                in_=x[bi].rearrange("(q c) j -> q (c j)", c=4),
-            )
-
-        load_item(0)
-        load_weights(0, o_xj)
-        load_item(1)
-        load_weights(1, rel_o_xj)
-        nc.sync.dma_start(
-            out=wraw[:, 2].rearrange("q d c n -> q d (c n)"),
-            in_=p_xj.rearrange("d (q c) n -> q d (c n)", c=4),
-        )
-        for k in range(1, XRING):
-            load_pair(k)
-
-        wgrp = const.tile([P, 3, P, 4], BF16, name="wgrp", align_bytes=64)
-        wcod = const.tile([P, 3 * P], U32, name="wcod", align_bytes=64)
-        wsc = const.tile([P, 3 * P], U8, name="wsc", align_bytes=64)
-
-        def quantise_weights(kind):
+        def quantise_w(kind):
+            grp = const.tile([P, P, 4], BF16, name="wgrp%d" % kind, align_bytes=64)
+            cod = const.tile([P, P], U32, name="wcod%d" % kind, align_bytes=64)
+            sc = const.tile([P, P], U8, name="wsc%d" % kind, align_bytes=64)
             nc.vector.tensor_copy(
-                out=wgrp[:, kind].rearrange("p (d n) t -> p d n t", d=ND),
-                in_=wraw[:, kind].rearrange("p d t n -> p d n t"),
+                out=grp[:].rearrange("p (d n) t -> p d n t", d=ND),
+                in_=wraw[kind][:].rearrange("p d t n -> p d n t"),
             )
             nc.vector.quantize_mx(
-                out=wcod[:, kind * P : (kind + 1) * P].bitcast(FP8X4),
-                scales=wsc[:, kind * P : (kind + 1) * P],
-                in_=wgrp[:, kind].rearrange("p w t -> p (w t)"),
+                out=cod[:].bitcast(FP8X4), scales=sc[:], in_=grp[:].rearrange("p w t -> p (w t)")
             )
-
-
-        def wslice(kind):
-            return (
-                wcod[:, kind * P : (kind + 1) * P].bitcast(FP8X4),
-                wsc[:, kind * P : (kind + 1) * P],
-            )
+            wq[kind] = (cod[:].bitcast(FP8X4), sc[:])
 
         xt = {}
         grp = {}
@@ -158,15 +173,16 @@ def tile_selfprojectiondev_pa_t_kernel(tc, x, o_xj, p_xj, rel_o_xj, out_0, out_1
                 banks.append(bank)
             xt[b] = banks
 
-        def evacuate(b):
-            g = gpool.tile([P, 4 * NI], BF16, name="grp", tag="grp", align_bytes=64)
-            grp[b] = g
-            g32 = g[:].bitcast(F32)
-            for h in range(2):
-                nc.scalar.copy(
-                    out=g32[:, h * 512 : (h + 1) * 512].rearrange("p (i u) -> p i u", u=2),
-                    in_=xt[b][h][:].rearrange("p u i -> p i u"),
-                )
+        def evacuate(b, h, eng):
+            if b not in grp:
+                grp[b] = gpool.tile([P, 4 * NI], BF16, name="grp", tag="grp", align_bytes=64)
+            g32 = grp[b][:].bitcast(F32)
+            dst = g32[:, h * 512 : (h + 1) * 512].rearrange("p (i u) -> p i u", u=2)
+            src = xt[b][h][:].rearrange("p u i -> p i u")
+            if eng == "s":
+                nc.scalar.copy(out=dst, in_=src)
+            else:
+                nc.vector.tensor_copy(out=dst, in_=src)
 
         def quantise_x(b):
             cod = cpool.tile([P, NI], U32, name="xcod", tag="xcod", align_bytes=64)
@@ -178,7 +194,7 @@ def tile_selfprojectiondev_pa_t_kernel(tc, x, o_xj, p_xj, rel_o_xj, out_0, out_1
             cod, sc = xc[b]
             z = ps_z.tile([P, 4, P], F32, name="zps", tag="zps")
             zt[b] = z
-            wc, ws = wslice(0)
+            wc, ws = wq[0]
             for c in range(4):
                 nc.tensor.matmul_mx(
                     out=z[:, c, :],
@@ -192,19 +208,18 @@ def tile_selfprojectiondev_pa_t_kernel(tc, x, o_xj, p_xj, rel_o_xj, out_0, out_1
 
         def matmul_r(b):
             cod, sc = xc[b]
-            r = ps_r.tile([P, NI], F32, name="rps", tag="rps")
+            r = ps_xt.tile([P, NI], F32, name="rps", tag="xtb")
             rt[b] = r
-            wc, ws = wslice(1)
-            for rep in range(DUP):
-                nc.tensor.matmul_mx(
-                    out=r[:],
-                    lhsT=wc,
-                    lhsT_scale=ws,
-                    rhs=cod[:].bitcast(FP8X4),
-                    rhs_scale=sc[:],
-                    start=True,
-                    stop=True,
-                )
+            wc, ws = wq[1]
+            nc.tensor.matmul_mx(
+                out=r[:],
+                lhsT=wc,
+                lhsT_scale=ws,
+                rhs=cod[:].bitcast(FP8X4),
+                rhs_scale=sc[:],
+                start=True,
+                stop=True,
+            )
 
         def row_max(b):
             nc.vector.tensor_reduce(
@@ -234,107 +249,103 @@ def tile_selfprojectiondev_pa_t_kernel(tc, x, o_xj, p_xj, rel_o_xj, out_0, out_1
 
         def stats_z(b):
             g, bl = b // 4, b % 4
-            if bl == 0:
-                st[g] = stpool.tile([P, 8, 6], F32, name="st", tag="st")
             for pair in range(ND // 2):
                 nc.vector.bn_stats(
-                    out=st[g][:, bl * 2 + pair, :],
+                    out=stz[:, b * 2 + pair, :],
                     in_=th[g][:, bl, pair * 256 : (pair + 1) * 256].rearrange("p (e w) -> p w e", e=2),
                 )
 
+        stp = {}
         me = {}
-        wk = {}
         rs = {}
         tg = {}
         tcd = {}
         ups = {}
         vv = {}
-        s12 = {}
+
         stp = {}
+        Z = (stz, sz, wz, 128.0, F_Z)
+        U = (stu, su, wu, 32.0, F_U)
 
-        def chain_tiles(key):
-            if key not in me:
-                me[key] = mepool.tile([P, 2, 32], F32, name="me", tag="me")
-                wk[key] = mepool.tile([P, 5, 32], F32, name="wk", tag="wk")
-                rs[key] = mepool.tile([P, 32], F32, name="rs", tag="rs")
-
-        sqms = {}
-
-        def square_means(g):
-            sv = st[g][:].rearrange("p k (h s) -> p k h s", s=3)
-            sqm = mepool.tile([P, 8, 2], F32, name="sqm", tag="sqm")
-            sqms[g] = sqm
-            nc.vector.tensor_tensor(out=sqm[:], in0=sv[:, :, :, 1], in1=sv[:, :, :, 1], op=ALU.mult)
-
-        def stats1_matmul(g):
-            sv = st[g][:].rearrange("p k (h s) -> p k h s", s=3)
-            ps = ps_st.tile([P, 2, 8, 2], F32, name="stps", tag="stps")
-            stp[g] = ps
-            nc.tensor.matmul(ps[:, 0], lhsT=negones128[:], rhs=sv[:, :, :, 1], start=True, stop=True)
-            nc.tensor.matmul(ps[:, 1], lhsT=ones16k[:], rhs=sv[:, :, :, 2], start=True, stop=False)
-            nc.tensor.matmul(ps[:, 1], lhsT=ones128[:], rhs=sqms[g][:], start=False, stop=True)
-
-        def stats1_out(g):
-            chain_tiles(g)
-            nc.vector.tensor_copy(
-                out=me[g][:, :, 0:16], in_=stp[g][:].rearrange("p k h s -> p k (h s)")
+        def means_squared(kind, lo, hi):
+            stt, s, weights, count, factor = kind
+            sv = stt[:].rearrange("p k (h s) -> p (k h) s", s=3)
+            nc.vector.scalar_tensor_tensor(
+                out=sv[:, lo:hi, 0], in0=sv[:, lo:hi, 1], scalar=count, in1=sv[:, lo:hi, 1], op0=ALU.mult, op1=ALU.mult
             )
 
-        def cols(k):
-            if k == NG:
-                return 16, 32
-            return 0, (20 if k >= KL else 16)
+        def sums(kind, lo, hi):
+            stt, s, weights, count, factor = kind
+            ps = ps_s.tile([P, 3, 32], F32, name="stps", tag="small")
+            stp[count, lo] = ps
+            sv = stt[:].rearrange("p k (h s) -> p s (k h)", s=3)
+            nc.tensor.matmul(ps[:, :, 0 : hi - lo], lhsT=weights[:], rhs=sv[:, :, lo:hi], start=True, stop=True)
 
-        def var_step(k, i):
-            c0, c1 = cols(k)
-            m, w = me[k], wk[k]
-            if i == 0:
-                nc.vector.tensor_tensor(out=w[:, 0, c0:c1], in0=m[:, 0, c0:c1], in1=m[:, 0, c0:c1], op=ALU.mult)
-            elif i == 1:
-                nc.vector.tensor_tensor(out=w[:, 1, c0:c1], in0=m[:, 1, c0:c1], in1=w[:, 0, c0:c1], op=ALU.max)
-            else:
-                nc.vector.tensor_tensor(out=w[:, 2, c0:c1], in0=w[:, 1, c0:c1], in1=w[:, 0, c0:c1], op=ALU.subtract)
+        def chain_mean(kind, lo, hi):
+            stt, s, weights, count, factor = kind
+            ps = stp[count, lo]
+            nc.scalar.activation(out=s[:, 0, lo:hi], in_=ps[:, 1, 0 : hi - lo], func=ACT.Copy, scale=-count)
+            nc.scalar.activation(out=s[:, 1, lo:hi], in_=ps[:, 1, 0 : hi - lo], func=ACT.Square, scale=count)
 
-        F_Z = 16384.0 / 16383.0
-        F_U = 1024.0 / 1023.0
+        def chain_sum(kind, lo, hi):
+            stt, s, weights, count, factor = kind
+            nc.vector.tensor_reduce(
+                out=s[:, 2, lo:hi],
+                in_=stp[count, lo][:, 0:3:2, 0 : hi - lo].rearrange("p s k -> p k s"),
+                axis=AX.X,
+                op=ALU.add,
+            )
+
+        def chain_max(kind, lo, hi):
+            s = kind[1]
+            nc.vector.tensor_tensor(out=s[:, 2, lo:hi], in0=s[:, 2, lo:hi], in1=s[:, 1, lo:hi], op=ALU.max)
+
+        def chain_var(kind, lo, hi):
+            s = kind[1]
+            nc.vector.tensor_tensor(out=s[:, 3, lo:hi], in0=s[:, 2, lo:hi], in1=s[:, 1, lo:hi], op=ALU.subtract)
+
+        def chain_root(kind, lo, hi):
+            stt, s, weights, count, factor = kind
+            nc.scalar.activation(out=s[:, 4, lo:hi], in_=s[:, 3, lo:hi], func=ACT.Sqrt, scale=factor)
+
+        def chain_pow(kind, lo, hi):
+            stt, s, weights, count, factor = kind
+            nc.gpsimd.tensor_tensor(out=s[:, 4, lo:hi], in0=s[:, 3, lo:hi], in1=half[:, 0 : hi - lo], op=ALU.pow)
+            nc.gpsimd.tensor_scalar(
+                out=s[:, 4, lo:hi], in0=s[:, 4, lo:hi], scalar1=factor**0.5, scalar2=EPS, op0=ALU.mult, op1=ALU.add
+            )
+
+        def chain_inv(kind, lo, hi):
+            s = kind[1]
+            nc.vector.reciprocal(out=s[:, 5, lo:hi], in_=s[:, 4, lo:hi])
+
+        def chain_recip(kind, lo, hi):
+            stt, s, weights, count, factor = kind
+            nc.vector.tensor_scalar(
+                out=s[:, 4, lo:hi], in0=s[:, 4, lo:hi], scalar1=EPS, scalar2=None, op0=ALU.add
+            )
+            nc.vector.reciprocal(out=s[:, 5, lo:hi], in_=s[:, 4, lo:hi])
+
+        def chain_bias(kind, lo, hi):
+            s = kind[1]
+            nc.vector.tensor_tensor(out=s[:, 6, lo:hi], in0=s[:, 0, lo:hi], in1=s[:, 5, lo:hi], op=ALU.mult)
 
         def warm(func):
             nc.scalar.activation(out=scratch[:], in_=half[:, 0:1], func=func)
 
-        def root(k):
-            c0, c1 = cols(k)
-            w = wk[k]
-            if k < NG - 1:
-                nc.gpsimd.tensor_tensor(out=w[:, 3, c0:c1], in0=w[:, 2, c0:c1], in1=half[:, c0:c1], op=ALU.pow)
-            else:
-                if c0 < 16:
-                    nc.scalar.activation(out=w[:, 3, c0:16], in_=w[:, 2, c0:16], func=ACT.Sqrt, scale=F_Z)
-                nc.scalar.activation(out=w[:, 3, 16:c1], in_=w[:, 2, 16:c1], func=ACT.Sqrt, scale=F_U)
-                nc.scalar.activation(out=w[:, 4, c0:c1], in_=w[:, 3, c0:c1], func=ACT.Copy, scale=1.0, bias=EPS)
-
-        def scale_std(k):
-            c0, c1 = cols(k)
-            w = wk[k]
-            nc.scalar.activation(out=w[:, 4, 0:16], in_=w[:, 3, 0:16], func=ACT.Copy, scale=F_Z ** 0.5, bias=EPS)
-            if c1 > 16:
-                nc.scalar.activation(out=w[:, 4, 16:c1], in_=w[:, 3, 16:c1], func=ACT.Copy, scale=F_U ** 0.5, bias=EPS)
-
-        def recip(k):
-            c0, c1 = cols(k)
-            nc.vector.reciprocal(out=rs[k][:, c0:c1], in_=wk[k][:, 4, c0:c1])
-
-        def standardise(g, bl):
-            if bl == 0:
+        def standardise(g, bl, d, engine):
+            if g not in tg:
                 tg[g] = tgpool.tile([P, 2048], BF16, name="tg", tag="tg", align_bytes=64)
-            for d in range(ND):
-                col = bl * 4 + d
-                nc.vector.tensor_scalar(
-                    out=tg[g][:, (d * 4 + bl) * P : (d * 4 + bl + 1) * P],
-                    in0=th[g][:, bl, d * P : (d + 1) * P],
-                    scalar1=me[g][:, 0, col : col + 1],
-                    scalar2=rs[g][:, col : col + 1],
-                    op0=ALU.add,
-                    op1=ALU.mult,
+            c = (4 * g + bl) * ND + d
+            out = tg[g][:, (d * 4 + bl) * P : (d * 4 + bl + 1) * P]
+            t = th[g][:, bl, d * P : (d + 1) * P]
+            if engine != "s":
+                (nc.vector if engine == "v" else nc.gpsimd).tensor_scalar(
+                    out=out, in0=t, scalar1=sz[:, 0, c : c + 1], scalar2=sz[:, 5, c : c + 1], op0=ALU.add, op1=ALU.mult
+                )
+            else:
+                nc.scalar.activation(
+                    out=out, in_=t, func=ACT.Identity, scale=sz[:, 5, c : c + 1], bias=sz[:, 6, c : c + 1]
                 )
 
         def quantise_t(g):
@@ -345,9 +356,9 @@ def tile_selfprojectiondev_pa_t_kernel(tc, x, o_xj, p_xj, rel_o_xj, out_0, out_1
 
         def matmul_u(g):
             cod, sc = tcd[g]
-            u = ps_u.tile([P, 16, NP], F32, name="ups", tag="ups")
+            u = ps_s.tile([P, 16, NP], F32, name="ups", tag="small")
             ups[g] = u
-            wc, ws = wslice(2)
+            wc, ws = wq[2]
             for d in range(ND):
                 nc.tensor.matmul_mx(
                     out=u[:, 4 * d : 4 * d + 4, :].rearrange("p k q -> p (k q)"),
@@ -360,48 +371,34 @@ def tile_selfprojectiondev_pa_t_kernel(tc, x, o_xj, p_xj, rel_o_xj, out_0, out_1
                 )
 
         def tanh_u(g):
-            v = vpool.tile([P, 2, ND, NP], F32, name="vv", tag="vv")
+            v = vpool.tile([P, ND, NP], F32, name="vv", tag="vv")
             vv[g] = v
-            nc.scalar.activation(out=v[:, 0], in_=ups[g][:, 0:16:5, :], func=ACT.Tanh)
-            nc.scalar.activation(out=v[:, 1], in_=v[:, 0], func=ACT.Square)
+            nc.scalar.activation(out=v[:], in_=ups[g][:, 0:16:5, :], func=ACT.Tanh)
 
-        def stats2_sum(g):
-            s = vpool.tile([P, 8], F32, name="s12", tag="s12")
-            s12[g] = s
-            nc.vector.tensor_reduce(
-                out=s[:], in_=vv[g][:].rearrange("p k d q -> p (k d) q"), axis=AX.X, op=ALU.add
-            )
-            ps = ps_st.tile([P, 8], F32, name="stps2", tag="stps")
-            stp[("u", g)] = ps
-            nc.tensor.matmul(ps[:, 0:4], lhsT=negbd1024[:], rhs=s[:, 0:4], start=True, stop=True)
-            nc.tensor.matmul(ps[:, 4:8], lhsT=bd1024[:], rhs=s[:, 4:8], start=True, stop=True)
-
-        def u_place(g):
-            if g + KL < NG:
-                return g + KL, 16
-            return NG, 16 + 4 * (g + KL - NG)
-
-        def stats2_out(g):
-            key, c0 = u_place(g)
-            chain_tiles(key)
-            nc.scalar.copy(
-                out=me[key][:, :, c0 : c0 + 4],
-                in_=stp[("u", g)][:].rearrange("p (k d) -> p k d", k=2),
-            )
-
-        def finish(g):
-            key, c0 = u_place(g)
-            ov = vpool.tile([P, ND, NP], F32, name="ov", tag="ov")
-            eng = nc.gpsimd if key < NG else nc.vector
-            for d in range(ND):
-                eng.tensor_scalar(
-                    out=ov[:, d, :],
-                    in0=vv[g][:, 0, d, :],
-                    scalar1=me[key][:, 0, c0 + d : c0 + d + 1],
-                    scalar2=rs[key][:, c0 + d : c0 + d + 1],
-                    op0=ALU.add,
-                    op1=ALU.mult,
+        def stats_u(g):
+            for pair in range(ND // 2):
+                nc.vector.bn_stats(
+                    out=stu[:, g * 2 + pair, :],
+                    in_=vv[g][:, 2 * pair : 2 * pair + 2, :].rearrange("p e q -> p q e"),
                 )
+
+        def finish(g, eng):
+            ov = vpool.tile([P, ND, NP], F32, name="ov", tag="ov")
+            for d in range(ND):
+                c = g * ND + d
+                if eng == "s":
+                    nc.scalar.activation(
+                        out=ov[:, d, :], in_=vv[g][:, d, :], func=ACT.Identity, scale=su[:, 5, c : c + 1], bias=su[:, 6, c : c + 1]
+                    )
+                else:
+                    (nc.vector if eng == "v" else nc.gpsimd).tensor_scalar(
+                        out=ov[:, d, :],
+                        in0=vv[g][:, d, :],
+                        scalar1=su[:, 0, c : c + 1],
+                        scalar2=su[:, 5, c : c + 1],
+                        op0=ALU.add,
+                        op1=ALU.mult,
+                    )
             for bl in range(4):
                 nc.sync.dma_start(
                     out=out_0[4 * g + bl].rearrange("d n q -> n d q"),
@@ -411,7 +408,7 @@ def tile_selfprojectiondev_pa_t_kernel(tc, x, o_xj, p_xj, rel_o_xj, out_0, out_1
         sm = {}
 
         def softmax_a():
-            tp = ps_xt.tile([P, 2, P], F32, name="smps", tag="xtb")
+            tp = ps_s.tile([P, 2, P], F32, name="smps", tag="small")
             sm["tp"] = tp
             nc.tensor.transpose(tp[:, 0, :], negmax[:], ident[:])
             nc.tensor.transpose(tp[:, 1, :], expsum[:], ident[:])
@@ -442,89 +439,155 @@ def tile_selfprojectiondev_pa_t_kernel(tc, x, o_xj, p_xj, rel_o_xj, out_0, out_1
             )
             nc.sync.dma_start(out=out_1[:, :, :], in_=mass[:])
 
-        def due(step, offset, count):
-            g, rem = divmod(step - FIRST - offset, 4)
-            return g if rem == 0 and 0 <= g < count else None
+        n = CHUNK * ND
+        chunks = [(Z, c * n, c * n + n) for c in range(NB // CHUNK)]
 
-        transposes(0)
-        for s in range(FIRST + 4 * (NG - 1) + 16):
-            rb = s - LAG
-            kp = due(s, 2, NG)
-            kf = due(s, 6, NG)
-            g0 = due(s, 0, NG)
-            if kf is not None and kf < NG - 1:
-                scale_std(kf)
+        def chunk(s, lag):
+            c, rem = divmod(s - lag, CHUNK)
+            return [chunks[c]] if rem == CHUNK - 1 and 0 <= c < len(chunks) else []
+
+        def first_phase(s):
+            on_vector = s % V_MOD in V_SET
             if s < NB:
-                evacuate(s)
+                if s == 0:
+                    evacuate(s, 0, "s")
+                evacuate(s, 1, "s")
+                if s > 0 and not on_vector:
+                    evacuate(s, 0, "s")
             if 0 <= s - 2 < NB:
                 tanh_z(s - 2)
-            g = due(s, 15, NG)
-            if g is not None:
-                stats2_out(g)
-            if s < 3:
-                quantise_weights(s)
+            if ROOT_S and s == NB + 1:
+                warm(ACT.Sqrt)
+            if s == 0:
+                quantise_w(0)
             if 0 <= s - 1 < NB:
                 quantise_x(s - 1)
-            if kp is not None:
-                var_step(kp, 0)
+            if s < NB and on_vector:
+                evacuate(s, 0, "v")
+            for a in chunk(s, 6):
+                chain_sum(*a)
+            if s in (4, 5):
+                quantise_w(s - 3)
             if 0 <= s - 3 < NB:
                 stats_z(s - 3)
-            if g0 is not None:
-                square_means(g0)
-            if kp is not None:
-                var_step(kp, 1)
-            if 0 <= rb < NB:
-                row_max(rb)
-                row_exp(rb)
-            if kp is not None:
-                var_step(kp, 2)
-                if kp == NG - 1:
-                    warm(ACT.Sqrt)
-                root(kp)
-                if kp == NG - 1:
-                    warm(ACT.Tanh)
-            if kf is not None:
-                recip(kf)
-            if 0 <= rb + 1 < NB:
-                matmul_r(rb + 1)
-            if s + 1 < NB:
-                transposes(s + 1)
-                if s % 2 == 0 and (s + 1) // 2 + XRING < NB // 2:
-                    load_pair((s + 1) // 2 + XRING)
+            for a in chunk(s, 6):
+                chain_max(*a)
+            for a in chunk(s, 7):
+                chain_var(*a)
+                if not ROOT_S:
+                    for lo in range(a[1], a[2], PW):
+                        chain_pow(Z, lo, lo + PW)
             if 0 <= s - 1 < NB:
                 matmul_z(s - 1)
-            if g0 is not None:
-                stats1_matmul(g0)
-            g = due(s, 10, NG)
-            if g is not None:
-                quantise_t(g)
-                matmul_u(g)
-            for bl in range(4):
-                g = due(s, 6 + bl, NG)
-                if g is not None:
-                    standardise(g, bl)
-            if kf is not None and kf >= KL:
-                finish(kf - KL)
-            g = due(s, 12, NG)
-            if g is not None:
-                tanh_u(g)
-                if g == NG - 1:
-                    warm(ACT.Sqrt)
-            g = due(s, 14, NG)
-            if g is not None:
-                stats2_sum(g)
-            g = due(s, 1, NG)
-            if g is not None:
-                stats1_out(g)
-            if s == FIRST + 4 * (NG - 1) + 3:
+            if s + T_AHEAD < NB:
+                transposes(s + T_AHEAD)
+            if s % 2 == 1 and s // 2 + XRING < NB // 2:
+                load_pair(s // 2 + XRING)
+            for a in chunk(s, 4):
+                sums(*a)
+            for a in chunk(s, 5):
+                chain_mean(*a)
+            for a in chunk(s, 3):
+                means_squared(*a)
+
+        for b in range(T_AHEAD):
+            transposes(b)
+        for s in range(NB + LEAD):
+            first_phase(s)
+        state = {"r": 0, "m": 0, "x": 0}
+
+        def product():
+            if state["r"] < NB:
+                matmul_r(state["r"])
+                state["r"] += 1
+
+        def maximum():
+            if state["m"] < state["r"]:
+                row_max(state["m"])
+                state["m"] += 1
+
+        def exponential():
+            if state["x"] < NB:
+                row_exp(state["x"])
+                state["x"] += 1
+
+        for i in range(R_AHEAD):
+            product()
+        for s in range(NB + LEAD, NB + 9):
+            if s in MAX_AT:
+                maximum()
+            first_phase(s)
+        if ROOT_S:
+            chain_root(Z, 0, nz)
+            warm(ACT.Exp)
+            for i in range(R_AHEAD - len(MAX_AT)):
+                maximum()
+            chain_recip(Z, 0, nz)
+            chain_bias(Z, 0, nz)
+        else:
+            chain_inv(Z, 0, INV * 16)
+            chain_bias(Z, 0, INV * 16)
+        calls = [(bl, d) for bl in range(4) for d in range(ND)]
+        work = {}
+
+        def put(q, what, fn, *args):
+            work.setdefault((q, what), []).append((fn, args))
+
+        def run(q, what):
+            for fn, args in work.get((q, what), []):
+                fn(*args)
+
+        for g in range(NG):
+            q0 = GS * g
+            engines = STD_V * ["v"] + STD_S * ["s"] + (16 - STD_V - STD_S) * ["g"]
+            by = {e: [c for c, x in zip(calls, ORDER16) if x == e] for e in "vsg"}
+            for e in "vsg":
+                for j, a in enumerate(by[e]):
+                    put(q0 + (j * GS) // len(by[e]), "std " + e, standardise, g, *a, e)
+            put(q0 + GS, "qt", quantise_t, g)
+            put(q0 + GS + 1, "u", matmul_u, g)
+            put(q0 + GS + 2, "tanh u", tanh_u, g)
+            put(q0 + GS + 3, "bn u", stats_u, g)
+        for lo, hi, q in UCH:
+            a = (U, 4 * lo, 4 * hi)
+            put(q, "sq", means_squared, *a)
+            put(q + 1, "sum", sums, *a)
+            put(q + 2, "mean", chain_mean, *a)
+            put(q + 3, "A", chain_sum, *a)
+            put(q + 3, "B", chain_max, *a)
+            put(q + 4, "B", chain_var, *a)
+            if not U_S:
+                put(q + 4, "B", chain_pow, *a)
+                put(q + 7, "A", chain_inv, *a)
+                for h in range(lo, hi):
+                    put(q + 7, "B", finish, h, "g" if h < NG - 2 else "v")
+        for q in range(NB + 10):
+            product()
+            run(q, "sum")
+            exponential()
+            run(q, "std s")
+            run(q, "std g")
+            run(q, "A")
+            run(q, "qt")
+            maximum()
+            run(q, "B")
+            run(q, "std v")
+            run(q, "bn u")
+            run(q, "sq")
+            run(q, "tanh u")
+            run(q, "mean")
+            run(q, "u")
+            if q == NB - 1:
                 softmax_a()
-            if s == FIRST + 4 * (NG - 1) + 10:
+                if U_S:
+                    warm(ACT.Sqrt)
+                    chain_root(U, 0, nu)
+                    warm(ACT.Exp)
                 softmax_b()
-            if s == FIRST + 4 * (NG - 1) + 11:
+                if U_S:
+                    chain_recip(U, 0, nu)
+                    chain_bias(U, 0, nu)
+                    for g in range(NG):
+                        finish(g, FIN[g])
+            if q == NB:
                 softmax_c()
-        for i in range(3):
-            var_step(NG, i)
-        root(NG)
-        recip(NG)
-        for g in range(NG - 1, NG - KL - 1, -1):
-            finish(g)

@@ -27,18 +27,19 @@ NG = NB // 4
 XRING = 5
 
 T_AHEAD = 2
-XT = 5
+XT = 4
 ZB = 2
-V_MOD, V_SET = 2, (1,)
-CHUNK = 4
+V_MOD, V_SET = 4, (1,)
+CHUNK = 8
 ROOT_S = True
 PW = 16
-LEAD = 2
-R_AHEAD = 4
+LEAD = 3
+R_AHEAD = 3
+PQ = 8
 GS = 3
 MAX_AT = (34, 35)
 STD_V, STD_S = 9, 7
-ORDER16 = "vsvsvvsvsvvsvsvs"
+ORDER16 = "svsvsvsvsvsvsvsv"
 UCH = ((0, 8, 27),)
 U_S = True
 FIN = ("v", "v", "s", "v", "g", "v", "s", "v")
@@ -59,7 +60,8 @@ def tile_selfprojectiondev_pa_t_kernel(tc, x, o_xj, p_xj, rel_o_xj, out_0, out_1
         jpool = ctx.enter_context(tc.tile_pool(name="jpool", bufs=2))
         ps_xt = ctx.enter_context(tc.psum_pool(name="ps_xt", bufs=XT))
         ps_z = ctx.enter_context(tc.psum_pool(name="ps_z", bufs=ZB))
-        ps_s = ctx.enter_context(tc.psum_pool(name="ps_s", bufs=8 - XT - ZB))
+        ps_s = ctx.enter_context(tc.psum_pool(name="ps_s", bufs=1))
+        ps_u = ctx.enter_context(tc.psum_pool(name="ps_u", bufs=1))
         ctx.enter_context(tc.manual_schedule())
 
         xs = {}
@@ -142,10 +144,17 @@ def tile_selfprojectiondev_pa_t_kernel(tc, x, o_xj, p_xj, rel_o_xj, out_0, out_1
             grp = const.tile([P, P, 4], BF16, name="wgrp%d" % kind, align_bytes=64)
             cod = const.tile([P, P], U32, name="wcod%d" % kind, align_bytes=64)
             sc = const.tile([P, P], U8, name="wsc%d" % kind, align_bytes=64)
-            nc.vector.tensor_copy(
-                out=grp[:].rearrange("p (d n) t -> p d n t", d=ND),
-                in_=wraw[kind][:].rearrange("p d t n -> p d n t"),
-            )
+            if kind == 0:
+                for h in range(2):
+                    nc.vector.tensor_copy(
+                        out=grp[:, 64 * h : 64 * h + 64].rearrange("p (n e) t -> p e n t", e=2),
+                        in_=wraw[kind][:, 2 * h : 2 * h + 2].rearrange("p e t n -> p e n t"),
+                    )
+            else:
+                nc.vector.tensor_copy(
+                    out=grp[:].rearrange("p (d n) t -> p d n t", d=ND),
+                    in_=wraw[kind][:].rearrange("p d t n -> p d n t"),
+                )
             nc.vector.quantize_mx(
                 out=cod[:].bitcast(FP8X4), scales=sc[:], in_=grp[:].rearrange("p w t -> p (w t)")
             )
@@ -242,8 +251,8 @@ def tile_selfprojectiondev_pa_t_kernel(tc, x, o_xj, p_xj, rel_o_xj, out_0, out_1
             if bl == 0:
                 th[g] = thpool.tile([P, 4, 512], F32, name="th", tag="th")
             nc.scalar.activation(
-                out=th[g][:, bl, :].rearrange("p (w c) -> p w c", c=4),
-                in_=zt[b][:].rearrange("p c w -> p w c"),
+                out=th[g][:, bl, :].rearrange("p (w c e) -> p w c e", c=4, e=2),
+                in_=zt[b][:].rearrange("p c (w e) -> p w c e", e=2),
                 func=ACT.Tanh,
             )
 
@@ -252,7 +261,7 @@ def tile_selfprojectiondev_pa_t_kernel(tc, x, o_xj, p_xj, rel_o_xj, out_0, out_1
             for pair in range(ND // 2):
                 nc.vector.bn_stats(
                     out=stz[:, b * 2 + pair, :],
-                    in_=th[g][:, bl, pair * 256 : (pair + 1) * 256].rearrange("p (e w) -> p w e", e=2),
+                    in_=th[g][:, bl, pair * 256 : (pair + 1) * 256],
                 )
 
         stp = {}
@@ -263,6 +272,7 @@ def tile_selfprojectiondev_pa_t_kernel(tc, x, o_xj, p_xj, rel_o_xj, out_0, out_1
         ups = {}
         vv = {}
 
+        stps = ps_s.tile([P, 3, 160], F32, name="stps")
         stp = {}
         Z = (stz, sz, wz, 128.0, F_Z)
         U = (stu, su, wu, 32.0, F_U)
@@ -276,10 +286,11 @@ def tile_selfprojectiondev_pa_t_kernel(tc, x, o_xj, p_xj, rel_o_xj, out_0, out_1
 
         def sums(kind, lo, hi):
             stt, s, weights, count, factor = kind
-            ps = ps_s.tile([P, 3, 32], F32, name="stps", tag="small")
+            off = 0 if count == 128 else 128
+            ps = stps[:, :, off + lo : off + hi]
             stp[count, lo] = ps
             sv = stt[:].rearrange("p k (h s) -> p s (k h)", s=3)
-            nc.tensor.matmul(ps[:, :, 0 : hi - lo], lhsT=weights[:], rhs=sv[:, :, lo:hi], start=True, stop=True)
+            nc.tensor.matmul(ps, lhsT=weights[:], rhs=sv[:, :, lo:hi], start=True, stop=True)
 
         def chain_mean(kind, lo, hi):
             stt, s, weights, count, factor = kind
@@ -338,7 +349,7 @@ def tile_selfprojectiondev_pa_t_kernel(tc, x, o_xj, p_xj, rel_o_xj, out_0, out_1
                 tg[g] = tgpool.tile([P, 2048], BF16, name="tg", tag="tg", align_bytes=64)
             c = (4 * g + bl) * ND + d
             out = tg[g][:, (d * 4 + bl) * P : (d * 4 + bl + 1) * P]
-            t = th[g][:, bl, d * P : (d + 1) * P]
+            t = th[g][:, bl, 256 * (d // 2) : 256 * (d // 2) + 256].rearrange("p (w e) -> p e w", e=2)[:, d % 2]
             if engine != "s":
                 (nc.vector if engine == "v" else nc.gpsimd).tensor_scalar(
                     out=out, in0=t, scalar1=sz[:, 0, c : c + 1], scalar2=sz[:, 5, c : c + 1], op0=ALU.add, op1=ALU.mult
@@ -356,7 +367,7 @@ def tile_selfprojectiondev_pa_t_kernel(tc, x, o_xj, p_xj, rel_o_xj, out_0, out_1
 
         def matmul_u(g):
             cod, sc = tcd[g]
-            u = ps_s.tile([P, 16, NP], F32, name="ups", tag="small")
+            u = ps_u.tile([P, 16, NP], F32, name="ups", tag="ups")
             ups[g] = u
             wc, ws = wq[2]
             for d in range(ND):
@@ -382,33 +393,38 @@ def tile_selfprojectiondev_pa_t_kernel(tc, x, o_xj, p_xj, rel_o_xj, out_0, out_1
                     in_=vv[g][:, 2 * pair : 2 * pair + 2, :].rearrange("p e q -> p q e"),
                 )
 
-        def finish(g, eng):
-            ov = vpool.tile([P, ND, NP], F32, name="ov", tag="ov")
-            for d in range(ND):
-                c = g * ND + d
-                if eng == "s":
-                    nc.scalar.activation(
-                        out=ov[:, d, :], in_=vv[g][:, d, :], func=ACT.Identity, scale=su[:, 5, c : c + 1], bias=su[:, 6, c : c + 1]
-                    )
-                else:
-                    (nc.vector if eng == "v" else nc.gpsimd).tensor_scalar(
-                        out=ov[:, d, :],
-                        in0=vv[g][:, d, :],
-                        scalar1=su[:, 0, c : c + 1],
-                        scalar2=su[:, 5, c : c + 1],
-                        op0=ALU.add,
-                        op1=ALU.mult,
-                    )
-            for bl in range(4):
-                nc.sync.dma_start(
-                    out=out_0[4 * g + bl].rearrange("d n q -> n d q"),
-                    in_=ov[32 * bl : 32 * bl + 32, :, :],
+        ov = const.tile([P, NG, ND, NP], F32, name="ov")
+
+        def finish(g, d, eng):
+            c = g * ND + d
+            if eng == "s":
+                nc.scalar.activation(
+                    out=ov[:, g, d, :],
+                    in_=vv[g][:, d, :],
+                    func=ACT.Identity,
+                    scale=su[:, 5, c : c + 1],
+                    bias=su[:, 6, c : c + 1],
                 )
+            else:
+                (nc.vector if eng == "v" else nc.gpsimd).tensor_scalar(
+                    out=ov[:, g, d, :],
+                    in0=vv[g][:, d, :],
+                    scalar1=su[:, 0, c : c + 1],
+                    scalar2=su[:, 5, c : c + 1],
+                    op0=ALU.add,
+                    op1=ALU.mult,
+                )
+
+        def store(bl, d):
+            (nc.sync if bl % 2 == 0 else nc.scalar).dma_start(
+                out=out_0.rearrange("(g l) d n q -> l d n g q", l=4)[bl, d],
+                in_=ov[32 * bl : 32 * bl + 32, :, d, :],
+            )
 
         sm = {}
 
         def softmax_a():
-            tp = ps_s.tile([P, 2, P], F32, name="smps", tag="small")
+            tp = ps_u.tile([P, 2, P], F32, name="smps", tag="ups")
             sm["tp"] = tp
             nc.tensor.transpose(tp[:, 0, :], negmax[:], ident[:])
             nc.tensor.transpose(tp[:, 1, :], expsum[:], ident[:])
@@ -465,7 +481,8 @@ def tile_selfprojectiondev_pa_t_kernel(tc, x, o_xj, p_xj, rel_o_xj, out_0, out_1
             if s < NB and on_vector:
                 evacuate(s, 0, "v")
             for a in chunk(s, 6):
-                chain_sum(*a)
+                if s <= NB:
+                    chain_sum(*a)
             if s in (4, 5):
                 quantise_w(s - 3)
             if 0 <= s - 3 < NB:
@@ -486,6 +503,8 @@ def tile_selfprojectiondev_pa_t_kernel(tc, x, o_xj, p_xj, rel_o_xj, out_0, out_1
             for a in chunk(s, 4):
                 sums(*a)
             for a in chunk(s, 5):
+                if s >= NB:
+                    chain_sum(*a)
                 chain_mean(*a)
             for a in chunk(s, 3):
                 means_squared(*a)
@@ -558,9 +577,8 @@ def tile_selfprojectiondev_pa_t_kernel(tc, x, o_xj, p_xj, rel_o_xj, out_0, out_1
             put(q + 4, "B", chain_var, *a)
             if not U_S:
                 put(q + 4, "B", chain_pow, *a)
-                put(q + 7, "A", chain_inv, *a)
-                for h in range(lo, hi):
-                    put(q + 7, "B", finish, h, "g" if h < NG - 2 else "v")
+                put(q + PQ, "A", chain_inv, *a)
+                pass
         for q in range(NB + 10):
             product()
             run(q, "sum")
@@ -587,7 +605,13 @@ def tile_selfprojectiondev_pa_t_kernel(tc, x, o_xj, p_xj, rel_o_xj, out_0, out_1
                 if U_S:
                     chain_recip(U, 0, nu)
                     chain_bias(U, 0, nu)
-                    for g in range(NG):
-                        finish(g, FIN[g])
+                    for d in range(ND):
+                        for g in range(NG):
+                            finish(g, d, FIN[g])
+                        store(0, d)
+                        store(2, d)
+                    for d in range(ND):
+                        store(1, d)
+                        store(3, d)
             if q == NB:
                 softmax_c()

@@ -36,13 +36,11 @@ PW = 16
 LEAD = 3
 R_AHEAD = 3
 PQ = 8
-GS = 3
+GS = 2
 MAX_AT = (34, 35)
 STD_V, STD_S = 9, 7
-ORDER16 = "svsvsvsvsvsvsvsv"
-UCH = ((0, 8, 27),)
-U_S = True
-FIN = ("v", "v", "s", "v", "g", "v", "s", "v")
+ORDER16 = "svsvssvsvssvsvsv"
+UCH = ((0, 3, 10, 19), (3, 6, 16, 25), (6, 8, 20, 29))
 INV, INV_AT = 5, 18
 
 
@@ -144,17 +142,10 @@ def tile_selfprojectiondev_pa_t_kernel(tc, x, o_xj, p_xj, rel_o_xj, out_0, out_1
             grp = const.tile([P, P, 4], BF16, name="wgrp%d" % kind, align_bytes=64)
             cod = const.tile([P, P], U32, name="wcod%d" % kind, align_bytes=64)
             sc = const.tile([P, P], U8, name="wsc%d" % kind, align_bytes=64)
-            if kind == 0:
-                for h in range(2):
-                    nc.vector.tensor_copy(
-                        out=grp[:, 64 * h : 64 * h + 64].rearrange("p (n e) t -> p e n t", e=2),
-                        in_=wraw[kind][:, 2 * h : 2 * h + 2].rearrange("p e t n -> p e n t"),
-                    )
-            else:
-                nc.vector.tensor_copy(
-                    out=grp[:].rearrange("p (d n) t -> p d n t", d=ND),
-                    in_=wraw[kind][:].rearrange("p d t n -> p d n t"),
-                )
+            nc.vector.tensor_copy(
+                out=grp[:].rearrange("p (d n) t -> p d n t", d=ND),
+                in_=wraw[kind][:].rearrange("p d t n -> p d n t"),
+            )
             nc.vector.quantize_mx(
                 out=cod[:].bitcast(FP8X4), scales=sc[:], in_=grp[:].rearrange("p w t -> p (w t)")
             )
@@ -251,8 +242,8 @@ def tile_selfprojectiondev_pa_t_kernel(tc, x, o_xj, p_xj, rel_o_xj, out_0, out_1
             if bl == 0:
                 th[g] = thpool.tile([P, 4, 512], F32, name="th", tag="th")
             nc.scalar.activation(
-                out=th[g][:, bl, :].rearrange("p (w c e) -> p w c e", c=4, e=2),
-                in_=zt[b][:].rearrange("p c (w e) -> p w c e", e=2),
+                out=th[g][:, bl, :].rearrange("p (w c) -> p w c", c=4),
+                in_=zt[b][:].rearrange("p c w -> p w c"),
                 func=ACT.Tanh,
             )
 
@@ -261,7 +252,7 @@ def tile_selfprojectiondev_pa_t_kernel(tc, x, o_xj, p_xj, rel_o_xj, out_0, out_1
             for pair in range(ND // 2):
                 nc.vector.bn_stats(
                     out=stz[:, b * 2 + pair, :],
-                    in_=th[g][:, bl, pair * 256 : (pair + 1) * 256],
+                    in_=th[g][:, bl, pair * 256 : (pair + 1) * 256].rearrange("p (e w) -> p w e", e=2),
                 )
 
         stp = {}
@@ -349,7 +340,7 @@ def tile_selfprojectiondev_pa_t_kernel(tc, x, o_xj, p_xj, rel_o_xj, out_0, out_1
                 tg[g] = tgpool.tile([P, 2048], BF16, name="tg", tag="tg", align_bytes=64)
             c = (4 * g + bl) * ND + d
             out = tg[g][:, (d * 4 + bl) * P : (d * 4 + bl + 1) * P]
-            t = th[g][:, bl, 256 * (d // 2) : 256 * (d // 2) + 256].rearrange("p (w e) -> p e w", e=2)[:, d % 2]
+            t = th[g][:, bl, d * P : (d + 1) * P]
             if engine != "s":
                 (nc.vector if engine == "v" else nc.gpsimd).tensor_scalar(
                     out=out, in0=t, scalar1=sz[:, 0, c : c + 1], scalar2=sz[:, 5, c : c + 1], op0=ALU.add, op1=ALU.mult
@@ -415,11 +406,17 @@ def tile_selfprojectiondev_pa_t_kernel(tc, x, o_xj, p_xj, rel_o_xj, out_0, out_1
                     op1=ALU.mult,
                 )
 
-        def store(bl, d):
-            (nc.sync if bl % 2 == 0 else nc.scalar).dma_start(
-                out=out_0.rearrange("(g l) d n q -> l d n g q", l=4)[bl, d],
-                in_=ov[32 * bl : 32 * bl + 32, :, d, :],
-            )
+        def store(g):
+            for bl in range(4):
+                nc.sync.dma_start(
+                    out=out_0[4 * g + bl].rearrange("d n q -> n d q"),
+                    in_=ov[32 * bl : 32 * bl + 32, g],
+                )
+
+        def finish_group(g, engines):
+            for d in range(ND):
+                finish(g, d, engines[d])
+            store(g)
 
         sm = {}
 
@@ -567,7 +564,7 @@ def tile_selfprojectiondev_pa_t_kernel(tc, x, o_xj, p_xj, rel_o_xj, out_0, out_1
             put(q0 + GS + 1, "u", matmul_u, g)
             put(q0 + GS + 2, "tanh u", tanh_u, g)
             put(q0 + GS + 3, "bn u", stats_u, g)
-        for lo, hi, q in UCH:
+        for lo, hi, q, later in UCH:
             a = (U, 4 * lo, 4 * hi)
             put(q, "sq", means_squared, *a)
             put(q + 1, "sum", sums, *a)
@@ -575,11 +572,14 @@ def tile_selfprojectiondev_pa_t_kernel(tc, x, o_xj, p_xj, rel_o_xj, out_0, out_1
             put(q + 3, "A", chain_sum, *a)
             put(q + 3, "B", chain_max, *a)
             put(q + 4, "B", chain_var, *a)
-            if not U_S:
-                put(q + 4, "B", chain_pow, *a)
-                put(q + PQ, "A", chain_inv, *a)
-                pass
+            put(q + 4, "B", chain_pow, *a)
+            put(later, "A", chain_inv, *a)
+            for h in range(lo, hi):
+                put(later, "C", finish_group, h, "gggg" if h < NG - 2 else "vvvv")
         for q in range(NB + 10):
+            if not ROOT_S and q == INV_AT:
+                chain_inv(Z, INV * 16, nz)
+                chain_bias(Z, INV * 16, nz)
             product()
             run(q, "sum")
             exponential()
@@ -595,23 +595,9 @@ def tile_selfprojectiondev_pa_t_kernel(tc, x, o_xj, p_xj, rel_o_xj, out_0, out_1
             run(q, "tanh u")
             run(q, "mean")
             run(q, "u")
+            run(q, "C")
             if q == NB - 1:
                 softmax_a()
-                if U_S:
-                    warm(ACT.Sqrt)
-                    chain_root(U, 0, nu)
-                    warm(ACT.Exp)
                 softmax_b()
-                if U_S:
-                    chain_recip(U, 0, nu)
-                    chain_bias(U, 0, nu)
-                    for d in range(ND):
-                        for g in range(NG):
-                            finish(g, d, FIN[g])
-                        store(0, d)
-                        store(2, d)
-                    for d in range(ND):
-                        store(1, d)
-                        store(3, d)
             if q == NB:
                 softmax_c()

@@ -34,13 +34,15 @@ CHUNK = 8
 ROOT_S = True
 PW = 16
 LEAD = 3
-R_AHEAD = 3
+R_AHEAD = 5
+R_FIRST = 3
+ESUM_FIRST = False
 PQ = 8
 GS = 2
-MAX_AT = (34, 35)
+MAX_AT = (34, 35, 36)
 STD_V, STD_S = 9, 7
 ORDER16 = "svsvssvsvssvsvsv"
-UCH = ((0, 3, 10, 19), (3, 6, 16, 25), (6, 8, 20, 29))
+UCH = ((0, 3, 10, 19), (3, 6, 16, 26), (6, 8, 20, 30))
 INV, INV_AT = 5, 18
 
 
@@ -208,7 +210,10 @@ def tile_selfprojectiondev_pa_t_kernel(tc, x, o_xj, p_xj, rel_o_xj, out_0, out_1
 
         def matmul_r(b):
             cod, sc = xc[b]
-            r = ps_xt.tile([P, NI], F32, name="rps", tag="xtb")
+            if b % 6 < 4:
+                r = ps_xt.tile([P, NI], F32, name="rps", tag="xtb")
+            else:
+                r = ps_z.tile([P, NI], F32, name="rps", tag="zps")
             rt[b] = r
             wc, ws = wq[1]
             nc.tensor.matmul_mx(
@@ -420,28 +425,26 @@ def tile_selfprojectiondev_pa_t_kernel(tc, x, o_xj, p_xj, rel_o_xj, out_0, out_1
 
         sm = {}
 
-        def softmax_a():
-            tp = ps_u.tile([P, 2, P], F32, name="smps", tag="ups")
-            sm["tp"] = tp
-            nc.tensor.transpose(tp[:, 0, :], negmax[:], ident[:])
-            nc.tensor.transpose(tp[:, 1, :], expsum[:], ident[:])
-
-        def softmax_b():
-            nmt = sm["tp"][0:NB, 0, :].rearrange("b (d n) -> b d n", d=ND)
+        def softmax_shares():
+            tp = ps_u.tile([P, P], F32, name="smps", tag="ups")
+            nc.tensor.transpose(tp[:], negmax[:], ident[:])
+            nmt = tp[0:NB, :].rearrange("b (d n) -> b d n", d=ND)
             gmin = const.tile([NB, ND], F32, name="gmin")
             nc.vector.tensor_reduce(out=gmin[:], in_=nmt, axis=AX.X, op=ALU.min)
             diff = const.tile([NB, ND, NP], F32, name="diff")
             nc.vector.tensor_tensor(
                 out=diff[:], in0=gmin[:].unsqueeze(2).to_broadcast([NB, ND, NP]), in1=nmt, op=ALU.subtract
             )
-            ex = const.tile([NB, ND, NP], F32, name="ex")
-            sm["ex"] = ex
-            nc.scalar.activation(out=ex[:], in_=diff[:], func=ACT.Exp)
+            sm["diff"] = diff
 
-        def softmax_c():
-            smt = sm["tp"][0:NB, 1, :].rearrange("b (d n) -> b d n", d=ND)
+        def softmax_mass():
+            ex = const.tile([NB, ND, NP], F32, name="ex")
+            nc.scalar.activation(out=ex[:], in_=sm["diff"][:], func=ACT.Exp)
+            tp = ps_u.tile([P, P], F32, name="smps", tag="ups")
+            nc.tensor.transpose(tp[:], expsum[:], ident[:])
+            smt = tp[0:NB, :].rearrange("b (d n) -> b d n", d=ND)
             wgt = const.tile([NB, ND, NP], F32, name="wgt")
-            nc.vector.tensor_tensor(out=wgt[:], in0=sm["ex"][:], in1=smt, op=ALU.mult)
+            nc.vector.tensor_tensor(out=wgt[:], in0=ex[:], in1=smt, op=ALU.mult)
             tot = const.tile([NB, ND], F32, name="tot")
             nc.vector.tensor_reduce(out=tot[:], in_=wgt[:], axis=AX.X, op=ALU.add)
             rtot = const.tile([NB, ND], F32, name="rtot")
@@ -500,9 +503,11 @@ def tile_selfprojectiondev_pa_t_kernel(tc, x, o_xj, p_xj, rel_o_xj, out_0, out_1
             for a in chunk(s, 4):
                 sums(*a)
             for a in chunk(s, 5):
-                if s >= NB:
+                if s >= NB and ESUM_FIRST:
                     chain_sum(*a)
                 chain_mean(*a)
+                if s >= NB and not ESUM_FIRST:
+                    chain_sum(*a)
             for a in chunk(s, 3):
                 means_squared(*a)
 
@@ -527,12 +532,14 @@ def tile_selfprojectiondev_pa_t_kernel(tc, x, o_xj, p_xj, rel_o_xj, out_0, out_1
                 row_exp(state["x"])
                 state["x"] += 1
 
-        for i in range(R_AHEAD):
+        for i in range(R_FIRST):
             product()
         for s in range(NB + LEAD, NB + 9):
             if s in MAX_AT:
                 maximum()
             first_phase(s)
+        for i in range(R_AHEAD - R_FIRST):
+            product()
         if ROOT_S:
             chain_root(Z, 0, nz)
             warm(ACT.Exp)
@@ -596,8 +603,7 @@ def tile_selfprojectiondev_pa_t_kernel(tc, x, o_xj, p_xj, rel_o_xj, out_0, out_1
             run(q, "mean")
             run(q, "u")
             run(q, "C")
+            if q == NB - R_AHEAD + 1:
+                softmax_shares()
             if q == NB - 1:
-                softmax_a()
-                softmax_b()
-            if q == NB:
-                softmax_c()
+                softmax_mass()

@@ -37,12 +37,12 @@ LEAD = 3
 R_AHEAD = 5
 R_FIRST = 3
 ESUM_FIRST = False
-PQ = 8
+FIN = ("vvvv",) * 8
 GS = 2
 MAX_AT = (34, 35, 36)
 STD_V, STD_S = 9, 7
 ORDER16 = "svsvssvsvssvsvsv"
-UCH = ((0, 3, 10, 19), (3, 6, 16, 26), (6, 8, 20, 30))
+UCH = ((0, 3, 10, 18), (3, 6, 16, 24), (6, 8, 20, 28))
 INV, INV_AT = 5, 18
 
 
@@ -582,7 +582,7 @@ def tile_selfprojectiondev_pa_t_kernel(tc, x, o_xj, p_xj, rel_o_xj, out_0, out_1
             put(q + 4, "B", chain_pow, *a)
             put(later, "A", chain_inv, *a)
             for h in range(lo, hi):
-                put(later, "C", finish_group, h, "gggg" if h < NG - 2 else "vvvv")
+                put(later, "C", finish_group, h, FIN[h])
         for q in range(NB + 10):
             if not ROOT_S and q == INV_AT:
                 chain_inv(Z, INV * 16, nz)

@@ -18,48 +18,40 @@ NI = 512
 NJ = 512
 NP = 32
 P = 128
+C = 4
 EPS = 1e-5
 FLOPS = 2 * NB * ND * (2 * NI * NJ * NP + NP * NI * NP)
 F_Z = (NI * NP) / (NI * NP - 1.0)
 F_U = (NP * NP) / (NP * NP - 1.0)
 
-NG = NB // 4
-XRING = 5
-
-T_AHEAD = 2
-XT = 4
-ZB = 2
-V_MOD, V_SET = 4, (1,)
+GROUP = 4
+NG = NB // GROUP
 CHUNK = 8
-ROOT_S = True
-PW = 16
-LEAD = 3
+X_PAIRS = 5
+V_COPY = 4
 R_AHEAD = 5
 R_FIRST = 3
-ESUM_FIRST = False
-FIN = ("vvvv",) * 8
-GS = 2
-MAX_AT = (34, 35, 36)
-STD_V, STD_S = 9, 7
-ORDER16 = "svsvssvsvssvsvsv"
-UCH = ((0, 3, 10, 18), (3, 6, 16, 24), (6, 8, 20, 28))
-INV, INV_AT = 5, 18
+SLOTS = 2
+CALLS = GROUP * ND
+CALLS_V = 7
+CHAIN = 10
+
+NEG_MEAN, MEAN_SQ, MEAN_OF_SQ, VAR, STD, INV_STD, SHIFT = range(7)
 
 
 def tile_selfprojectiondev_pa_t_kernel(tc, x, o_xj, p_xj, rel_o_xj, out_0, out_1):
     nc = tc.nc
     with ExitStack() as ctx:
         const = ctx.enter_context(tc.tile_pool(name="const", bufs=1))
-        xpool = ctx.enter_context(tc.tile_pool(name="xpool", bufs=XRING))
+        xpool = ctx.enter_context(tc.tile_pool(name="xpool", bufs=X_PAIRS))
         gpool = ctx.enter_context(tc.tile_pool(name="gpool", bufs=3))
         cpool = ctx.enter_context(tc.tile_pool(name="cpool", bufs=NB))
         thpool = ctx.enter_context(tc.tile_pool(name="thpool", bufs=NG))
-        smpool = ctx.enter_context(tc.tile_pool(name="smpool", bufs=8))
         tgpool = ctx.enter_context(tc.tile_pool(name="tgpool", bufs=2))
         vpool = ctx.enter_context(tc.tile_pool(name="vpool", bufs=NG))
         jpool = ctx.enter_context(tc.tile_pool(name="jpool", bufs=2))
-        ps_xt = ctx.enter_context(tc.psum_pool(name="ps_xt", bufs=XT))
-        ps_z = ctx.enter_context(tc.psum_pool(name="ps_z", bufs=ZB))
+        ps_xt = ctx.enter_context(tc.psum_pool(name="ps_xt", bufs=4))
+        ps_z = ctx.enter_context(tc.psum_pool(name="ps_z", bufs=2))
         ps_s = ctx.enter_context(tc.psum_pool(name="ps_s", bufs=1))
         ps_u = ctx.enter_context(tc.psum_pool(name="ps_u", bufs=1))
         ctx.enter_context(tc.manual_schedule())
@@ -67,7 +59,7 @@ def tile_selfprojectiondev_pa_t_kernel(tc, x, o_xj, p_xj, rel_o_xj, out_0, out_1
         xs = {}
 
         def x_tile(k):
-            xs[k] = xpool.tile([P, 2, 4, NJ], BF16, name="xs", tag="xs")
+            xs[k] = xpool.tile([P, 2, C, NJ], BF16, name="xs", tag="xs")
 
         def load_half_item(k, bi, h):
             nc.sync.dma_start(
@@ -78,17 +70,18 @@ def tile_selfprojectiondev_pa_t_kernel(tc, x, o_xj, p_xj, rel_o_xj, out_0, out_1
         def load_item(k, bi):
             nc.sync.dma_start(
                 out=xs[k][:, bi].rearrange("q c j -> q (c j)"),
-                in_=x[2 * k + bi].rearrange("(q c) j -> q (c j)", c=4),
+                in_=x[2 * k + bi].rearrange("(q c) j -> q (c j)", c=C),
             )
 
         def load_pair(k):
             x_tile(k)
             nc.sync.dma_start(
                 out=xs[k][:].rearrange("q b c j -> q b (c j)"),
-                in_=x[2 * k : 2 * k + 2].rearrange("b (q c) j -> q b (c j)", c=4),
+                in_=x[2 * k : 2 * k + 2].rearrange("b (q c) j -> q b (c j)", c=C),
             )
 
-        wraw = [const.tile([P, ND, 4, NP], BF16, name="wraw%d" % k) for k in range(3)]
+        O_XJ, REL_O_XJ, P_XJ = range(3)
+        wraw = [const.tile([P, ND, C, NP], BF16, name="wraw%d" % k) for k in range(3)]
 
         def load_w(kind, w):
             wv = w.rearrange("d (u p e) n -> u p d (e n)", u=2, p=P, e=2)
@@ -101,47 +94,50 @@ def tile_selfprojectiondev_pa_t_kernel(tc, x, o_xj, p_xj, rel_o_xj, out_0, out_1
         x_tile(0)
         load_half_item(0, 0, 0)
         load_half_item(0, 0, 1)
-        load_w(0, o_xj)
+        load_w(O_XJ, o_xj)
         load_item(0, 1)
         x_tile(1)
         load_item(1, 0)
         load_item(1, 1)
         load_pair(2)
-        load_w(1, rel_o_xj)
+        load_w(REL_O_XJ, rel_o_xj)
         nc.sync.dma_start(
-            out=wraw[2][:].rearrange("q d c n -> q d (c n)"),
-            in_=p_xj.rearrange("d (q c) n -> q d (c n)", c=4),
+            out=wraw[P_XJ][:].rearrange("q d c n -> q d (c n)"),
+            in_=p_xj.rearrange("d (q c) n -> q d (c n)", c=C),
         )
-        for k in range(3, XRING):
+        for k in range(3, X_PAIRS):
             load_pair(k)
 
-        half = const.tile([P, 32], F32, name="half")
+        half = const.tile([P, 3 * ND], F32, name="half")
         nc.vector.memset(half[:], 0.5)
         scratch = const.tile([P, 1], F32, name="scratch")
-        nc.scalar.activation(out=scratch[:], in_=half[:, 0:1], func=ACT.Tanh)
+
+        def load_table(func):
+            nc.scalar.activation(out=scratch[:], in_=half[:, 0:1], func=func)
+
+        load_table(ACT.Tanh)
         ident = const.tile([P, P], F32, name="ident")
         make_identity(nc, ident[:])
         wz = const.tile([P, P], F32, name="wz")
-        nc.vector.memset(wz[:], 1.0 / 16384.0)
+        nc.vector.memset(wz[:], 1.0 / (P * P))
         wu = const.tile([P, P], F32, name="wu")
         nc.vector.memset(wu[:], 0.0)
-        for q in range(4):
-            block = slice(32 * q, 32 * q + 32)
-            nc.vector.memset(wu[block, block], 1.0 / 1024.0)
+        for q in range(GROUP):
+            block = slice(NP * q, NP * q + NP)
+            nc.vector.memset(wu[block, block], 1.0 / (NP * NP))
         negmax = const.tile([P, P], F32, name="negmax")
         nc.vector.memset(negmax[:], 0.0)
         expsum = const.tile([P, P], F32, name="expsum")
         nc.vector.memset(expsum[:], 0.0)
 
-        stz = const.tile([P, NB * 2, 6], F32, name="stz")
-        stu = const.tile([P, NG * 2, 6], F32, name="stu")
-        nz, nu = NB * ND, NG * ND
-        sz = const.tile([P, 7, nz], F32, name="sz")
-        su = const.tile([P, 7, nu], F32, name="su")
-        wq = {}
+        stz = const.tile([P, NB * ND // 2, 6], F32, name="stz")
+        stu = const.tile([P, NG * ND // 2, 6], F32, name="stu")
+        sz = const.tile([P, 7, NB * ND], F32, name="sz")
+        su = const.tile([P, 7, NG * ND], F32, name="su")
+        weights = {}
 
         def quantise_w(kind):
-            grp = const.tile([P, P, 4], BF16, name="wgrp%d" % kind, align_bytes=64)
+            grp = const.tile([P, P, C], BF16, name="wgrp%d" % kind, align_bytes=64)
             cod = const.tile([P, P], U32, name="wcod%d" % kind, align_bytes=64)
             sc = const.tile([P, P], U8, name="wsc%d" % kind, align_bytes=64)
             nc.vector.tensor_copy(
@@ -151,21 +147,19 @@ def tile_selfprojectiondev_pa_t_kernel(tc, x, o_xj, p_xj, rel_o_xj, out_0, out_1
             nc.vector.quantize_mx(
                 out=cod[:].bitcast(FP8X4), scales=sc[:], in_=grp[:].rearrange("p w t -> p (w t)")
             )
-            wq[kind] = (cod[:].bitcast(FP8X4), sc[:])
+            weights[kind] = (cod[:].bitcast(FP8X4), sc[:])
 
         xt = {}
         grp = {}
         xc = {}
         zt = {}
-        rt = {}
         th = {}
-        st = {}
 
         def transposes(b):
             pair = xs[b // 2]
             banks = []
             for h in range(2):
-                bank = ps_xt.tile([P, 2, 256], F32, name="xtb", tag="xtb")
+                bank = ps_xt.tile([P, 2, 2 * P], F32, name="xtb", tag="xtb")
                 for cc in range(2):
                     xw = pair[:, b % 2, 2 * h + cc, :].bitcast(F32)
                     for u in range(2):
@@ -175,16 +169,14 @@ def tile_selfprojectiondev_pa_t_kernel(tc, x, o_xj, p_xj, rel_o_xj, out_0, out_1
                 banks.append(bank)
             xt[b] = banks
 
-        def evacuate(b, h, eng):
+        def copy_half(b, h, copy):
             if b not in grp:
-                grp[b] = gpool.tile([P, 4 * NI], BF16, name="grp", tag="grp", align_bytes=64)
+                grp[b] = gpool.tile([P, C * NI], BF16, name="grp", tag="grp", align_bytes=64)
             g32 = grp[b][:].bitcast(F32)
-            dst = g32[:, h * 512 : (h + 1) * 512].rearrange("p (i u) -> p i u", u=2)
-            src = xt[b][h][:].rearrange("p u i -> p i u")
-            if eng == "s":
-                nc.scalar.copy(out=dst, in_=src)
-            else:
-                nc.vector.tensor_copy(out=dst, in_=src)
+            copy(
+                out=g32[:, h * NI : (h + 1) * NI].rearrange("p (i u) -> p i u", u=2),
+                in_=xt[b][h][:].rearrange("p u i -> p i u"),
+            )
 
         def quantise_x(b):
             cod = cpool.tile([P, NI], U32, name="xcod", tag="xcod", align_bytes=64)
@@ -194,10 +186,10 @@ def tile_selfprojectiondev_pa_t_kernel(tc, x, o_xj, p_xj, rel_o_xj, out_0, out_1
 
         def matmul_z(b):
             cod, sc = xc[b]
-            z = ps_z.tile([P, 4, P], F32, name="zps", tag="zps")
+            z = ps_z.tile([P, C, P], F32, name="zps", tag="zps")
             zt[b] = z
-            wc, ws = wq[0]
-            for c in range(4):
+            wc, ws = weights[O_XJ]
+            for c in range(C):
                 nc.tensor.matmul_mx(
                     out=z[:, c, :],
                     lhsT=cod[:, c * P : (c + 1) * P].bitcast(FP8X4),
@@ -208,14 +200,186 @@ def tile_selfprojectiondev_pa_t_kernel(tc, x, o_xj, p_xj, rel_o_xj, out_0, out_1
                     stop=True,
                 )
 
-        def matmul_r(b):
-            cod, sc = xc[b]
+        def tanh_z(b):
+            g, bl = b // GROUP, b % GROUP
+            if bl == 0:
+                th[g] = thpool.tile([P, GROUP, C * P], F32, name="th", tag="th")
+            nc.scalar.activation(
+                out=th[g][:, bl, :].rearrange("p (w c) -> p w c", c=C),
+                in_=zt[b][:].rearrange("p c w -> p w c"),
+                func=ACT.Tanh,
+            )
+
+        def stats_z(b):
+            g, bl = b // GROUP, b % GROUP
+            for k in range(ND // 2):
+                nc.vector.bn_stats(
+                    out=stz[:, b * (ND // 2) + k, :],
+                    in_=th[g][:, bl, k * 2 * P : (k + 1) * 2 * P].rearrange("p (e w) -> p w e", e=2),
+                )
+
+        Z = (stz, sz, wz, float(P), F_Z, 0)
+        U = (stu, su, wu, float(NP), F_U, NB * ND)
+        totals = ps_s.tile([P, 3, NB * ND + NG * ND], F32, name="totals")
+
+        def place_squares(kind, lo, hi):
+            values, table, sum_w, n, factor, col = kind
+            v = values[:].rearrange("p k (h s) -> p (k h) s", s=3)[:, lo:hi]
+            nc.vector.scalar_tensor_tensor(
+                out=v[:, :, 0], in0=v[:, :, 1], scalar=n, in1=v[:, :, 1], op0=ALU.mult, op1=ALU.mult
+            )
+
+        def sums(kind, lo, hi):
+            values, table, sum_w, n, factor, col = kind
+            nc.tensor.matmul(
+                totals[:, :, col + lo : col + hi],
+                lhsT=sum_w[:],
+                rhs=values[:].rearrange("p k (h s) -> p s (k h)", s=3)[:, :, lo:hi],
+                start=True,
+                stop=True,
+            )
+
+        def means(kind, lo, hi):
+            values, table, sum_w, n, factor, col = kind
+            total = totals[:, 1, col + lo : col + hi]
+            nc.scalar.activation(out=table[:, NEG_MEAN, lo:hi], in_=total, func=ACT.Copy, scale=-n)
+            nc.scalar.activation(out=table[:, MEAN_SQ, lo:hi], in_=total, func=ACT.Square, scale=n)
+
+        def mean_of_squares(kind, lo, hi):
+            values, table, sum_w, n, factor, col = kind
+            nc.vector.tensor_reduce(
+                out=table[:, MEAN_OF_SQ, lo:hi],
+                in_=totals[:, 0:3:2, col + lo : col + hi].rearrange("p s k -> p k s"),
+                axis=AX.X,
+                op=ALU.add,
+            )
+
+        def no_less(kind, lo, hi):
+            row = kind[1][:, MEAN_OF_SQ, lo:hi]
+            nc.vector.tensor_tensor(out=row, in0=row, in1=kind[1][:, MEAN_SQ, lo:hi], op=ALU.max)
+
+        def variance(kind, lo, hi):
+            table = kind[1]
+            nc.vector.tensor_tensor(
+                out=table[:, VAR, lo:hi],
+                in0=table[:, MEAN_OF_SQ, lo:hi],
+                in1=table[:, MEAN_SQ, lo:hi],
+                op=ALU.subtract,
+            )
+
+        def all_roots_z():
+            nc.scalar.activation(out=sz[:, STD, :], in_=sz[:, VAR, :], func=ACT.Sqrt, scale=F_Z)
+
+        def inverses_z():
+            nc.vector.tensor_scalar(out=sz[:, STD, :], in0=sz[:, STD, :], scalar1=EPS, scalar2=None, op0=ALU.add)
+            nc.vector.reciprocal(out=sz[:, INV_STD, :], in_=sz[:, STD, :])
+            nc.vector.tensor_tensor(
+                out=sz[:, SHIFT, :], in0=sz[:, NEG_MEAN, :], in1=sz[:, INV_STD, :], op=ALU.mult
+            )
+
+        def roots_u(lo, hi):
+            row = su[:, STD, lo:hi]
+            nc.gpsimd.tensor_tensor(out=row, in0=su[:, VAR, lo:hi], in1=half[:, 0 : hi - lo], op=ALU.pow)
+            nc.gpsimd.tensor_scalar(
+                out=row, in0=row, scalar1=F_U**0.5, scalar2=EPS, op0=ALU.mult, op1=ALU.add
+            )
+
+        def inverses_u(lo, hi):
+            nc.vector.reciprocal(out=su[:, INV_STD, lo:hi], in_=su[:, STD, lo:hi])
+
+        tg = {}
+        tcd = {}
+        ups = {}
+        tu = {}
+
+        def standardise(g, bl, d, on_vector):
+            if g not in tg:
+                tg[g] = tgpool.tile([P, ND * GROUP * P], BF16, name="tg", tag="tg", align_bytes=64)
+            k = (GROUP * g + bl) * ND + d
+            out = tg[g][:, (d * GROUP + bl) * P : (d * GROUP + bl + 1) * P]
+            t = th[g][:, bl, d * P : (d + 1) * P]
+            inv_std = sz[:, INV_STD, k : k + 1]
+            if on_vector:
+                nc.vector.tensor_scalar(
+                    out=out,
+                    in0=t,
+                    scalar1=sz[:, NEG_MEAN, k : k + 1],
+                    scalar2=inv_std,
+                    op0=ALU.add,
+                    op1=ALU.mult,
+                )
+            else:
+                nc.scalar.activation(
+                    out=out, in_=t, func=ACT.Identity, scale=inv_std, bias=sz[:, SHIFT, k : k + 1]
+                )
+
+        def quantise_t(g):
+            cod = tgpool.tile([P, ND * P], U32, name="tcod", tag="tcod", align_bytes=64)
+            sc = tgpool.tile([P, ND * P], U8, name="tsc", tag="tsc", align_bytes=64)
+            tcd[g] = (cod, sc)
+            nc.vector.quantize_mx(out=cod[:].bitcast(FP8X4), scales=sc[:], in_=tg[g][:])
+
+        def matmul_u(g):
+            cod, sc = tcd[g]
+            u = ps_u.tile([P, ND * ND, NP], F32, name="ups", tag="ups")
+            ups[g] = u
+            wc, ws = weights[P_XJ]
+            for d in range(ND):
+                nc.tensor.matmul_mx(
+                    out=u[:, ND * d : ND * d + ND, :].rearrange("p k q -> p (k q)"),
+                    lhsT=cod[:, d * P : (d + 1) * P].bitcast(FP8X4),
+                    lhsT_scale=sc[:, d * P : (d + 1) * P],
+                    rhs=wc,
+                    rhs_scale=ws,
+                    start=True,
+                    stop=True,
+                )
+
+        def tanh_u(g):
+            tu[g] = vpool.tile([P, ND, NP], F32, name="tu", tag="tu")
+            nc.scalar.activation(out=tu[g][:], in_=ups[g][:, 0 : ND * ND : ND + 1, :], func=ACT.Tanh)
+
+        def stats_u(g):
+            for k in range(ND // 2):
+                nc.vector.bn_stats(
+                    out=stu[:, g * (ND // 2) + k, :],
+                    in_=tu[g][:, 2 * k : 2 * k + 2, :].rearrange("p e q -> p q e"),
+                )
+
+        proj = const.tile([P, NG, ND, NP], F32, name="proj")
+
+        def finish(g):
+            for d in range(ND):
+                k = g * ND + d
+                nc.vector.tensor_scalar(
+                    out=proj[:, g, d, :],
+                    in0=tu[g][:, d, :],
+                    scalar1=su[:, NEG_MEAN, k : k + 1],
+                    scalar2=su[:, INV_STD, k : k + 1],
+                    op0=ALU.add,
+                    op1=ALU.mult,
+                )
+            for bl in range(GROUP):
+                nc.sync.dma_start(
+                    out=out_0[GROUP * g + bl].rearrange("d n q -> n d q"),
+                    in_=proj[NP * bl : NP * bl + NP, g],
+                )
+
+        rt = {}
+        done = {"product": 0, "maximum": 0, "exponential": 0}
+
+        def product():
+            b = done["product"]
+            if b == NB:
+                return
+            done["product"] += 1
             if b % 6 < 4:
                 r = ps_xt.tile([P, NI], F32, name="rps", tag="xtb")
             else:
                 r = ps_z.tile([P, NI], F32, name="rps", tag="zps")
             rt[b] = r
-            wc, ws = wq[1]
+            cod, sc = xc[b]
+            wc, ws = weights[REL_O_XJ]
             nc.tensor.matmul_mx(
                 out=r[:],
                 lhsT=wc,
@@ -226,12 +390,18 @@ def tile_selfprojectiondev_pa_t_kernel(tc, x, o_xj, p_xj, rel_o_xj, out_0, out_1
                 stop=True,
             )
 
-        def row_max(b):
+        def maximum():
+            b = done["maximum"]
+            if b == NB:
+                return
+            done["maximum"] += 1
             nc.vector.tensor_reduce(
                 out=negmax[:, b : b + 1], in_=rt[b][:], axis=AX.X, op=ALU.max, negate=True
             )
 
-        def row_exp(b):
+        def exponential():
+            b = done["exponential"]
+            done["exponential"] += 1
             junk = jpool.tile([P, NI], BF16, name="junk", tag="junk")
             nc.scalar.activation(
                 out=junk[:],
@@ -242,368 +412,155 @@ def tile_selfprojectiondev_pa_t_kernel(tc, x, o_xj, p_xj, rel_o_xj, out_0, out_1
                 accum_out=expsum[:, b : b + 1],
             )
 
-        def tanh_z(b):
-            g, bl = b // 4, b % 4
-            if bl == 0:
-                th[g] = thpool.tile([P, 4, 512], F32, name="th", tag="th")
-            nc.scalar.activation(
-                out=th[g][:, bl, :].rearrange("p (w c) -> p w c", c=4),
-                in_=zt[b][:].rearrange("p c w -> p w c"),
-                func=ACT.Tanh,
-            )
+        def by_item(values):
+            turned = ps_u.tile([P, P], F32, name="turned", tag="ups")
+            nc.tensor.transpose(turned[:], values[:], ident[:])
+            return turned[0:NB, :].rearrange("b (d n) -> b d n", d=ND)
 
-        def stats_z(b):
-            g, bl = b // 4, b % 4
-            for pair in range(ND // 2):
-                nc.vector.bn_stats(
-                    out=stz[:, b * 2 + pair, :],
-                    in_=th[g][:, bl, pair * 256 : (pair + 1) * 256].rearrange("p (e w) -> p w e", e=2),
-                )
+        diff = const.tile([NB, ND, NP], F32, name="diff")
 
-        stp = {}
-        me = {}
-        rs = {}
-        tg = {}
-        tcd = {}
-        ups = {}
-        vv = {}
-
-        stps = ps_s.tile([P, 3, 160], F32, name="stps")
-        stp = {}
-        Z = (stz, sz, wz, 128.0, F_Z)
-        U = (stu, su, wu, 32.0, F_U)
-
-        def means_squared(kind, lo, hi):
-            stt, s, weights, count, factor = kind
-            sv = stt[:].rearrange("p k (h s) -> p (k h) s", s=3)
-            nc.vector.scalar_tensor_tensor(
-                out=sv[:, lo:hi, 0], in0=sv[:, lo:hi, 1], scalar=count, in1=sv[:, lo:hi, 1], op0=ALU.mult, op1=ALU.mult
-            )
-
-        def sums(kind, lo, hi):
-            stt, s, weights, count, factor = kind
-            off = 0 if count == 128 else 128
-            ps = stps[:, :, off + lo : off + hi]
-            stp[count, lo] = ps
-            sv = stt[:].rearrange("p k (h s) -> p s (k h)", s=3)
-            nc.tensor.matmul(ps, lhsT=weights[:], rhs=sv[:, :, lo:hi], start=True, stop=True)
-
-        def chain_mean(kind, lo, hi):
-            stt, s, weights, count, factor = kind
-            ps = stp[count, lo]
-            nc.scalar.activation(out=s[:, 0, lo:hi], in_=ps[:, 1, 0 : hi - lo], func=ACT.Copy, scale=-count)
-            nc.scalar.activation(out=s[:, 1, lo:hi], in_=ps[:, 1, 0 : hi - lo], func=ACT.Square, scale=count)
-
-        def chain_sum(kind, lo, hi):
-            stt, s, weights, count, factor = kind
-            nc.vector.tensor_reduce(
-                out=s[:, 2, lo:hi],
-                in_=stp[count, lo][:, 0:3:2, 0 : hi - lo].rearrange("p s k -> p k s"),
-                axis=AX.X,
-                op=ALU.add,
-            )
-
-        def chain_max(kind, lo, hi):
-            s = kind[1]
-            nc.vector.tensor_tensor(out=s[:, 2, lo:hi], in0=s[:, 2, lo:hi], in1=s[:, 1, lo:hi], op=ALU.max)
-
-        def chain_var(kind, lo, hi):
-            s = kind[1]
-            nc.vector.tensor_tensor(out=s[:, 3, lo:hi], in0=s[:, 2, lo:hi], in1=s[:, 1, lo:hi], op=ALU.subtract)
-
-        def chain_root(kind, lo, hi):
-            stt, s, weights, count, factor = kind
-            nc.scalar.activation(out=s[:, 4, lo:hi], in_=s[:, 3, lo:hi], func=ACT.Sqrt, scale=factor)
-
-        def chain_pow(kind, lo, hi):
-            stt, s, weights, count, factor = kind
-            nc.gpsimd.tensor_tensor(out=s[:, 4, lo:hi], in0=s[:, 3, lo:hi], in1=half[:, 0 : hi - lo], op=ALU.pow)
-            nc.gpsimd.tensor_scalar(
-                out=s[:, 4, lo:hi], in0=s[:, 4, lo:hi], scalar1=factor**0.5, scalar2=EPS, op0=ALU.mult, op1=ALU.add
-            )
-
-        def chain_inv(kind, lo, hi):
-            s = kind[1]
-            nc.vector.reciprocal(out=s[:, 5, lo:hi], in_=s[:, 4, lo:hi])
-
-        def chain_recip(kind, lo, hi):
-            stt, s, weights, count, factor = kind
-            nc.vector.tensor_scalar(
-                out=s[:, 4, lo:hi], in0=s[:, 4, lo:hi], scalar1=EPS, scalar2=None, op0=ALU.add
-            )
-            nc.vector.reciprocal(out=s[:, 5, lo:hi], in_=s[:, 4, lo:hi])
-
-        def chain_bias(kind, lo, hi):
-            s = kind[1]
-            nc.vector.tensor_tensor(out=s[:, 6, lo:hi], in0=s[:, 0, lo:hi], in1=s[:, 5, lo:hi], op=ALU.mult)
-
-        def warm(func):
-            nc.scalar.activation(out=scratch[:], in_=half[:, 0:1], func=func)
-
-        def standardise(g, bl, d, engine):
-            if g not in tg:
-                tg[g] = tgpool.tile([P, 2048], BF16, name="tg", tag="tg", align_bytes=64)
-            c = (4 * g + bl) * ND + d
-            out = tg[g][:, (d * 4 + bl) * P : (d * 4 + bl + 1) * P]
-            t = th[g][:, bl, d * P : (d + 1) * P]
-            if engine != "s":
-                (nc.vector if engine == "v" else nc.gpsimd).tensor_scalar(
-                    out=out, in0=t, scalar1=sz[:, 0, c : c + 1], scalar2=sz[:, 5, c : c + 1], op0=ALU.add, op1=ALU.mult
-                )
-            else:
-                nc.scalar.activation(
-                    out=out, in_=t, func=ACT.Identity, scale=sz[:, 5, c : c + 1], bias=sz[:, 6, c : c + 1]
-                )
-
-        def quantise_t(g):
-            cod = tgpool.tile([P, 512], U32, name="tcod", tag="tcod", align_bytes=64)
-            sc = tgpool.tile([P, 512], U8, name="tsc", tag="tsc", align_bytes=64)
-            tcd[g] = (cod, sc)
-            nc.vector.quantize_mx(out=cod[:].bitcast(FP8X4), scales=sc[:], in_=tg[g][:])
-
-        def matmul_u(g):
-            cod, sc = tcd[g]
-            u = ps_u.tile([P, 16, NP], F32, name="ups", tag="ups")
-            ups[g] = u
-            wc, ws = wq[2]
-            for d in range(ND):
-                nc.tensor.matmul_mx(
-                    out=u[:, 4 * d : 4 * d + 4, :].rearrange("p k q -> p (k q)"),
-                    lhsT=cod[:, d * P : (d + 1) * P].bitcast(FP8X4),
-                    lhsT_scale=sc[:, d * P : (d + 1) * P],
-                    rhs=wc,
-                    rhs_scale=ws,
-                    start=True,
-                    stop=True,
-                )
-
-        def tanh_u(g):
-            v = vpool.tile([P, ND, NP], F32, name="vv", tag="vv")
-            vv[g] = v
-            nc.scalar.activation(out=v[:], in_=ups[g][:, 0:16:5, :], func=ACT.Tanh)
-
-        def stats_u(g):
-            for pair in range(ND // 2):
-                nc.vector.bn_stats(
-                    out=stu[:, g * 2 + pair, :],
-                    in_=vv[g][:, 2 * pair : 2 * pair + 2, :].rearrange("p e q -> p q e"),
-                )
-
-        ov = const.tile([P, NG, ND, NP], F32, name="ov")
-
-        def finish(g, d, eng):
-            c = g * ND + d
-            if eng == "s":
-                nc.scalar.activation(
-                    out=ov[:, g, d, :],
-                    in_=vv[g][:, d, :],
-                    func=ACT.Identity,
-                    scale=su[:, 5, c : c + 1],
-                    bias=su[:, 6, c : c + 1],
-                )
-            else:
-                (nc.vector if eng == "v" else nc.gpsimd).tensor_scalar(
-                    out=ov[:, g, d, :],
-                    in0=vv[g][:, d, :],
-                    scalar1=su[:, 0, c : c + 1],
-                    scalar2=su[:, 5, c : c + 1],
-                    op0=ALU.add,
-                    op1=ALU.mult,
-                )
-
-        def store(g):
-            for bl in range(4):
-                nc.sync.dma_start(
-                    out=out_0[4 * g + bl].rearrange("d n q -> n d q"),
-                    in_=ov[32 * bl : 32 * bl + 32, g],
-                )
-
-        def finish_group(g, engines):
-            for d in range(ND):
-                finish(g, d, engines[d])
-            store(g)
-
-        sm = {}
-
-        def softmax_shares():
-            tp = ps_u.tile([P, P], F32, name="smps", tag="ups")
-            nc.tensor.transpose(tp[:], negmax[:], ident[:])
-            nmt = tp[0:NB, :].rearrange("b (d n) -> b d n", d=ND)
-            gmin = const.tile([NB, ND], F32, name="gmin")
-            nc.vector.tensor_reduce(out=gmin[:], in_=nmt, axis=AX.X, op=ALU.min)
-            diff = const.tile([NB, ND, NP], F32, name="diff")
+        def below_largest():
+            nmt = by_item(negmax)
+            least = const.tile([NB, ND], F32, name="least")
+            nc.vector.tensor_reduce(out=least[:], in_=nmt, axis=AX.X, op=ALU.min)
             nc.vector.tensor_tensor(
-                out=diff[:], in0=gmin[:].unsqueeze(2).to_broadcast([NB, ND, NP]), in1=nmt, op=ALU.subtract
+                out=diff[:], in0=least[:].unsqueeze(2).to_broadcast([NB, ND, NP]), in1=nmt, op=ALU.subtract
             )
-            sm["diff"] = diff
 
-        def softmax_mass():
-            ex = const.tile([NB, ND, NP], F32, name="ex")
-            nc.scalar.activation(out=ex[:], in_=sm["diff"][:], func=ACT.Exp)
-            tp = ps_u.tile([P, P], F32, name="smps", tag="ups")
-            nc.tensor.transpose(tp[:], expsum[:], ident[:])
-            smt = tp[0:NB, :].rearrange("b (d n) -> b d n", d=ND)
-            wgt = const.tile([NB, ND, NP], F32, name="wgt")
-            nc.vector.tensor_tensor(out=wgt[:], in0=ex[:], in1=smt, op=ALU.mult)
-            tot = const.tile([NB, ND], F32, name="tot")
-            nc.vector.tensor_reduce(out=tot[:], in_=wgt[:], axis=AX.X, op=ALU.add)
-            rtot = const.tile([NB, ND], F32, name="rtot")
-            nc.vector.reciprocal(out=rtot[:], in_=tot[:])
+        def finish_softmax():
+            share = const.tile([NB, ND, NP], F32, name="share")
+            nc.scalar.activation(out=share[:], in_=diff[:], func=ACT.Exp)
+            weighted = const.tile([NB, ND, NP], F32, name="weighted")
+            nc.vector.tensor_tensor(out=weighted[:], in0=share[:], in1=by_item(expsum), op=ALU.mult)
+            total = const.tile([NB, ND], F32, name="total")
+            nc.vector.tensor_reduce(out=total[:], in_=weighted[:], axis=AX.X, op=ALU.add)
+            inverse = const.tile([NB, ND], F32, name="inverse")
+            nc.vector.reciprocal(out=inverse[:], in_=total[:])
             mass = const.tile([NB, ND, NP], F32, name="mass")
             nc.vector.tensor_tensor(
-                out=mass[:], in0=wgt[:], in1=rtot[:].unsqueeze(2).to_broadcast([NB, ND, NP]), op=ALU.mult
+                out=mass[:],
+                in0=weighted[:],
+                in1=inverse[:].unsqueeze(2).to_broadcast([NB, ND, NP]),
+                op=ALU.mult,
             )
             nc.sync.dma_start(out=out_1[:, :, :], in_=mass[:])
 
-        n = CHUNK * ND
-        chunks = [(Z, c * n, c * n + n) for c in range(NB // CHUNK)]
-
-        def chunk(s, lag):
+        def chunk_due(s, lag):
             c, rem = divmod(s - lag, CHUNK)
-            return [chunks[c]] if rem == CHUNK - 1 and 0 <= c < len(chunks) else []
+            if rem == CHUNK - 1 and 0 <= c < NB // CHUNK:
+                return [(Z, c * CHUNK * ND, (c + 1) * CHUNK * ND)]
+            return []
 
-        def first_phase(s):
-            on_vector = s % V_MOD in V_SET
-            if s < NB:
-                if s == 0:
-                    evacuate(s, 0, "s")
-                evacuate(s, 1, "s")
-                if s > 0 and not on_vector:
-                    evacuate(s, 0, "s")
+        transposes(0)
+        transposes(1)
+        for s in range(NB + 3):
+            if s == 0:
+                copy_half(s, 0, nc.scalar.copy)
+                copy_half(s, 1, nc.scalar.copy)
+            elif s < NB:
+                copy_half(s, 1, nc.scalar.copy)
+                if s % V_COPY != 1:
+                    copy_half(s, 0, nc.scalar.copy)
             if 0 <= s - 2 < NB:
                 tanh_z(s - 2)
-            if ROOT_S and s == NB + 1:
-                warm(ACT.Sqrt)
+            if s == NB + 1:
+                load_table(ACT.Sqrt)
             if s == 0:
-                quantise_w(0)
+                quantise_w(O_XJ)
             if 0 <= s - 1 < NB:
                 quantise_x(s - 1)
-            if s < NB and on_vector:
-                evacuate(s, 0, "v")
-            for a in chunk(s, 6):
-                if s <= NB:
-                    chain_sum(*a)
-            if s in (4, 5):
-                quantise_w(s - 3)
-            if 0 <= s - 3 < NB:
+            if s < NB and s % V_COPY == 1:
+                copy_half(s, 0, nc.vector.tensor_copy)
+            for chunk in chunk_due(s, 6):
+                mean_of_squares(*chunk)
+            if s == 4:
+                quantise_w(REL_O_XJ)
+            if s == 5:
+                quantise_w(P_XJ)
+            if s >= 3:
                 stats_z(s - 3)
-            for a in chunk(s, 6):
-                chain_max(*a)
-            for a in chunk(s, 7):
-                chain_var(*a)
-                if not ROOT_S:
-                    for lo in range(a[1], a[2], PW):
-                        chain_pow(Z, lo, lo + PW)
+            for chunk in chunk_due(s, 6):
+                no_less(*chunk)
+            for chunk in chunk_due(s, 7):
+                variance(*chunk)
             if 0 <= s - 1 < NB:
                 matmul_z(s - 1)
-            if s + T_AHEAD < NB:
-                transposes(s + T_AHEAD)
-            if s % 2 == 1 and s // 2 + XRING < NB // 2:
-                load_pair(s // 2 + XRING)
-            for a in chunk(s, 4):
-                sums(*a)
-            for a in chunk(s, 5):
-                if s >= NB and ESUM_FIRST:
-                    chain_sum(*a)
-                chain_mean(*a)
-                if s >= NB and not ESUM_FIRST:
-                    chain_sum(*a)
-            for a in chunk(s, 3):
-                means_squared(*a)
+            if s + 2 < NB:
+                transposes(s + 2)
+            if s % 2 == 1 and s // 2 + X_PAIRS < NB // 2:
+                load_pair(s // 2 + X_PAIRS)
+            for chunk in chunk_due(s, 4):
+                sums(*chunk)
+            for chunk in chunk_due(s, 5):
+                means(*chunk)
+            for chunk in chunk_due(s, 3):
+                place_squares(*chunk)
 
-        for b in range(T_AHEAD):
-            transposes(b)
-        for s in range(NB + LEAD):
-            first_phase(s)
-        state = {"r": 0, "m": 0, "x": 0}
-
-        def product():
-            if state["r"] < NB:
-                matmul_r(state["r"])
-                state["r"] += 1
-
-        def maximum():
-            if state["m"] < state["r"]:
-                row_max(state["m"])
-                state["m"] += 1
-
-        def exponential():
-            if state["x"] < NB:
-                row_exp(state["x"])
-                state["x"] += 1
-
-        for i in range(R_FIRST):
+        last = (Z, (NB - CHUNK) * ND, NB * ND)
+        for _ in range(R_FIRST):
             product()
-        for s in range(NB + LEAD, NB + 9):
-            if s in MAX_AT:
-                maximum()
-            first_phase(s)
-        for i in range(R_AHEAD - R_FIRST):
+        maximum()
+        sums(*last)
+        maximum()
+        means(*last)
+        mean_of_squares(*last)
+        no_less(*last)
+        variance(*last)
+        for _ in range(R_AHEAD - R_FIRST):
             product()
-        if ROOT_S:
-            chain_root(Z, 0, nz)
-            warm(ACT.Exp)
-            for i in range(R_AHEAD - len(MAX_AT)):
-                maximum()
-            chain_recip(Z, 0, nz)
-            chain_bias(Z, 0, nz)
-        else:
-            chain_inv(Z, 0, INV * 16)
-            chain_bias(Z, 0, INV * 16)
-        calls = [(bl, d) for bl in range(4) for d in range(ND)]
+        all_roots_z()
+        load_table(ACT.Exp)
+        maximum()
+        maximum()
+        inverses_z()
+
         work = {}
 
-        def put(q, what, fn, *args):
-            work.setdefault((q, what), []).append((fn, args))
+        def put(q, place, fn, *args):
+            work.setdefault((q, place), []).append((fn, args))
 
-        def run(q, what):
-            for fn, args in work.get((q, what), []):
+        def run(q, place):
+            for fn, args in work.get((q, place), []):
                 fn(*args)
 
         for g in range(NG):
-            q0 = GS * g
-            engines = STD_V * ["v"] + STD_S * ["s"] + (16 - STD_V - STD_S) * ["g"]
-            by = {e: [c for c, x in zip(calls, ORDER16) if x == e] for e in "vsg"}
-            for e in "vsg":
-                for j, a in enumerate(by[e]):
-                    put(q0 + (j * GS) // len(by[e]), "std " + e, standardise, g, *a, e)
-            put(q0 + GS, "qt", quantise_t, g)
-            put(q0 + GS + 1, "u", matmul_u, g)
-            put(q0 + GS + 2, "tanh u", tanh_u, g)
-            put(q0 + GS + 3, "bn u", stats_u, g)
-        for lo, hi, q, later in UCH:
-            a = (U, 4 * lo, 4 * hi)
-            put(q, "sq", means_squared, *a)
-            put(q + 1, "sum", sums, *a)
-            put(q + 2, "mean", chain_mean, *a)
-            put(q + 3, "A", chain_sum, *a)
-            put(q + 3, "B", chain_max, *a)
-            put(q + 4, "B", chain_var, *a)
-            put(q + 4, "B", chain_pow, *a)
-            put(later, "A", chain_inv, *a)
-            for h in range(lo, hi):
-                put(later, "C", finish_group, h, FIN[h])
-        for q in range(NB + 10):
-            if not ROOT_S and q == INV_AT:
-                chain_inv(Z, INV * 16, nz)
-                chain_bias(Z, INV * 16, nz)
+            q = SLOTS * g
+            for k in range(CALLS):
+                on_vector = (CALLS_V * (k + 1) + CALLS // 2) // CALLS > (CALLS_V * k + CALLS // 2) // CALLS
+                place = "vector" if on_vector else "scalar"
+                put(q + k * SLOTS // CALLS, place, standardise, g, k // ND, k % ND, on_vector)
+            put(q + SLOTS, "quantise", quantise_t, g)
+            put(q + SLOTS + 1, "u", matmul_u, g)
+            put(q + SLOTS + 2, "tanh", tanh_u, g)
+            put(q + SLOTS + 3, "after maximum", stats_u, g)
+        for lo, hi in ((0, 3), (3, 6), (6, NG)):
+            q = SLOTS * (hi - 1) + SLOTS + 5
+            cols = (ND * lo, ND * hi)
+            put(q, "after maximum", place_squares, U, *cols)
+            put(q + 1, "sums", sums, U, *cols)
+            put(q + 2, "tanh", means, U, *cols)
+            put(q + 3, "before maximum", mean_of_squares, U, *cols)
+            put(q + 3, "behind maximum", no_less, U, *cols)
+            put(q + 4, "behind maximum", variance, U, *cols)
+            put(q + 4, "behind maximum", roots_u, *cols)
+            put(q + CHAIN, "before maximum", inverses_u, *cols)
+            for g in range(lo, hi):
+                put(q + CHAIN, "end", finish, g)
+
+        for q in range(NB):
             product()
-            run(q, "sum")
+            run(q, "sums")
             exponential()
-            run(q, "std s")
-            run(q, "std g")
-            run(q, "A")
-            run(q, "qt")
+            run(q, "scalar")
+            run(q, "before maximum")
+            run(q, "quantise")
             maximum()
-            run(q, "B")
-            run(q, "std v")
-            run(q, "bn u")
-            run(q, "sq")
-            run(q, "tanh u")
-            run(q, "mean")
+            run(q, "behind maximum")
+            run(q, "vector")
+            run(q, "after maximum")
+            run(q, "tanh")
             run(q, "u")
-            run(q, "C")
+            run(q, "end")
             if q == NB - R_AHEAD + 1:
-                softmax_shares()
-            if q == NB - 1:
-                softmax_mass()
+                below_largest()
+        finish_softmax()

from contextlib import ExitStack

import concourse.mybir as mybir
from concourse.masks import make_identity

F32 = mybir.dt.float32
BF16 = mybir.dt.bfloat16
U32 = mybir.dt.uint32
U8 = mybir.dt.uint8
FP8X4 = mybir.dt.float8_e4m3fn_x4
ACT = mybir.ActivationFunctionType
ALU = mybir.AluOpType
AX = mybir.AxisListType

NB = 32
ND = 4
NI = 512
NJ = 512
NP = 32
P = 128
C = 4
EPS = 1e-5
FLOPS = 2 * NB * ND * (2 * NI * NJ * NP + NP * NI * NP)
F_Z = (NI * NP) / (NI * NP - 1.0)
F_U = (NP * NP) / (NP * NP - 1.0)

GROUP = 4
NG = NB // GROUP
CHUNK = 8
X_PAIRS = 5
V_COPY = 4
R_AHEAD = 5
R_FIRST = 3
SLOTS = 2
CALLS = GROUP * ND
CALLS_V = 7
CHAIN = 10

NEG_MEAN, MEAN_SQ, MEAN_OF_SQ, VAR, STD, INV_STD, SHIFT = range(7)


def tile_selfprojectiondev_pa_t_kernel(tc, x, o_xj, p_xj, rel_o_xj, out_0, out_1):
    nc = tc.nc
    with ExitStack() as ctx:
        const = ctx.enter_context(tc.tile_pool(name="const", bufs=1))
        xpool = ctx.enter_context(tc.tile_pool(name="xpool", bufs=X_PAIRS))
        gpool = ctx.enter_context(tc.tile_pool(name="gpool", bufs=3))
        cpool = ctx.enter_context(tc.tile_pool(name="cpool", bufs=NB))
        thpool = ctx.enter_context(tc.tile_pool(name="thpool", bufs=NG))
        tgpool = ctx.enter_context(tc.tile_pool(name="tgpool", bufs=2))
        vpool = ctx.enter_context(tc.tile_pool(name="vpool", bufs=NG))
        jpool = ctx.enter_context(tc.tile_pool(name="jpool", bufs=2))
        ps_xt = ctx.enter_context(tc.psum_pool(name="ps_xt", bufs=4))
        ps_z = ctx.enter_context(tc.psum_pool(name="ps_z", bufs=2))
        ps_s = ctx.enter_context(tc.psum_pool(name="ps_s", bufs=1))
        ps_u = ctx.enter_context(tc.psum_pool(name="ps_u", bufs=1))
        ctx.enter_context(tc.manual_schedule())

        xs = {}

        def x_tile(k):
            xs[k] = xpool.tile([P, 2, C, NJ], BF16, name="xs", tag="xs")

        def load_half_item(k, bi, h):
            nc.sync.dma_start(
                out=xs[k][:, bi, 2 * h : 2 * h + 2].rearrange("q c j -> q (c j)"),
                in_=x[2 * k + bi].rearrange("(q h c) j -> h q (c j)", h=2, c=2)[h],
            )

        def load_item(k, bi):
            nc.sync.dma_start(
                out=xs[k][:, bi].rearrange("q c j -> q (c j)"),
                in_=x[2 * k + bi].rearrange("(q c) j -> q (c j)", c=C),
            )

        def load_pair(k):
            x_tile(k)
            nc.sync.dma_start(
                out=xs[k][:].rearrange("q b c j -> q b (c j)"),
                in_=x[2 * k : 2 * k + 2].rearrange("b (q c) j -> q b (c j)", c=C),
            )

        O_XJ, REL_O_XJ, P_XJ = range(3)
        wraw = [const.tile([P, ND, C, NP], BF16, name="wraw%d" % k) for k in range(3)]

        def load_w(kind, w):
            wv = w.rearrange("d (u p e) n -> u p d (e n)", u=2, p=P, e=2)
            for u in range(2):
                nc.sync.dma_start(
                    out=wraw[kind][:, :, 2 * u : 2 * u + 2, :].rearrange("p d e n -> p d (e n)"),
                    in_=wv[u],
                )

        x_tile(0)
        load_half_item(0, 0, 0)
        load_half_item(0, 0, 1)
        load_w(O_XJ, o_xj)
        load_item(0, 1)
        x_tile(1)
        load_item(1, 0)
        load_item(1, 1)
        load_pair(2)
        load_w(REL_O_XJ, rel_o_xj)
        nc.sync.dma_start(
            out=wraw[P_XJ][:].rearrange("q d c n -> q d (c n)"),
            in_=p_xj.rearrange("d (q c) n -> q d (c n)", c=C),
        )
        for k in range(3, X_PAIRS):
            load_pair(k)

        half = const.tile([P, 3 * ND], F32, name="half")
        nc.vector.memset(half[:], 0.5)
        scratch = const.tile([P, 1], F32, name="scratch")

        def load_table(func):
            nc.scalar.activation(out=scratch[:], in_=half[:, 0:1], func=func)

        load_table(ACT.Tanh)
        ident = const.tile([P, P], F32, name="ident")
        make_identity(nc, ident[:])
        wz = const.tile([P, P], F32, name="wz")
        nc.vector.memset(wz[:], 1.0 / (P * P))
        wu = const.tile([P, P], F32, name="wu")
        nc.vector.memset(wu[:], 0.0)
        for q in range(GROUP):
            block = slice(NP * q, NP * q + NP)
            nc.vector.memset(wu[block, block], 1.0 / (NP * NP))
        negmax = const.tile([P, P], F32, name="negmax")
        nc.vector.memset(negmax[:], 0.0)
        expsum = const.tile([P, P], F32, name="expsum")
        nc.vector.memset(expsum[:], 0.0)

        stz = const.tile([P, NB * ND // 2, 6], F32, name="stz")
        stu = const.tile([P, NG * ND // 2, 6], F32, name="stu")
        sz = const.tile([P, 7, NB * ND], F32, name="sz")
        su = const.tile([P, 7, NG * ND], F32, name="su")
        weights = {}

        def quantise_w(kind):
            grp = const.tile([P, P, C], BF16, name="wgrp%d" % kind, align_bytes=64)
            cod = const.tile([P, P], U32, name="wcod%d" % kind, align_bytes=64)
            sc = const.tile([P, P], U8, name="wsc%d" % kind, align_bytes=64)
            nc.vector.tensor_copy(
                out=grp[:].rearrange("p (d n) t -> p d n t", d=ND),
                in_=wraw[kind][:].rearrange("p d t n -> p d n t"),
            )
            nc.vector.quantize_mx(
                out=cod[:].bitcast(FP8X4), scales=sc[:], in_=grp[:].rearrange("p w t -> p (w t)")
            )
            weights[kind] = (cod[:].bitcast(FP8X4), sc[:])

        xt = {}
        grp = {}
        xc = {}
        zt = {}
        th = {}

        def transposes(b):
            pair = xs[b // 2]
            banks = []
            for h in range(2):
                bank = ps_xt.tile([P, 2, 2 * P], F32, name="xtb", tag="xtb")
                for cc in range(2):
                    xw = pair[:, b % 2, 2 * h + cc, :].bitcast(F32)
                    for u in range(2):
                        nc.tensor.transpose(
                            bank[:, u, cc * P : (cc + 1) * P], xw[:, u * P : (u + 1) * P], ident[:]
                        )
                banks.append(bank)
            xt[b] = banks

        def copy_half(b, h, copy):
            if b not in grp:
                grp[b] = gpool.tile([P, C * NI], BF16, name="grp", tag="grp", align_bytes=64)
            g32 = grp[b][:].bitcast(F32)
            copy(
                out=g32[:, h * NI : (h + 1) * NI].rearrange("p (i u) -> p i u", u=2),
                in_=xt[b][h][:].rearrange("p u i -> p i u"),
            )

        def quantise_x(b):
            cod = cpool.tile([P, NI], U32, name="xcod", tag="xcod", align_bytes=64)
            sc = cpool.tile([P, NI], U8, name="xsc", tag="xsc", align_bytes=64)
            xc[b] = (cod, sc)
            nc.vector.quantize_mx(out=cod[:].bitcast(FP8X4), scales=sc[:], in_=grp[b][:])

        def matmul_z(b):
            cod, sc = xc[b]
            z = ps_z.tile([P, C, P], F32, name="zps", tag="zps")
            zt[b] = z
            wc, ws = weights[O_XJ]
            for c in range(C):
                nc.tensor.matmul_mx(
                    out=z[:, c, :],
                    lhsT=cod[:, c * P : (c + 1) * P].bitcast(FP8X4),
                    lhsT_scale=sc[:, c * P : (c + 1) * P],
                    rhs=wc,
                    rhs_scale=ws,
                    start=True,
                    stop=True,
                )

        def tanh_z(b):
            g, bl = b // GROUP, b % GROUP
            if bl == 0:
                th[g] = thpool.tile([P, GROUP, C * P], F32, name="th", tag="th")
            nc.scalar.activation(
                out=th[g][:, bl, :].rearrange("p (w c) -> p w c", c=C),
                in_=zt[b][:].rearrange("p c w -> p w c"),
                func=ACT.Tanh,
            )

        def stats_z(b):
            g, bl = b // GROUP, b % GROUP
            for k in range(ND // 2):
                nc.vector.bn_stats(
                    out=stz[:, b * (ND // 2) + k, :],
                    in_=th[g][:, bl, k * 2 * P : (k + 1) * 2 * P].rearrange("p (e w) -> p w e", e=2),
                )

        Z = (stz, sz, wz, float(P), F_Z, 0)
        U = (stu, su, wu, float(NP), F_U, NB * ND)
        totals = ps_s.tile([P, 3, NB * ND + NG * ND], F32, name="totals")

        def place_squares(kind, lo, hi):
            values, table, sum_w, n, factor, col = kind
            v = values[:].rearrange("p k (h s) -> p (k h) s", s=3)[:, lo:hi]
            nc.vector.scalar_tensor_tensor(
                out=v[:, :, 0], in0=v[:, :, 1], scalar=n, in1=v[:, :, 1], op0=ALU.mult, op1=ALU.mult
            )

        def sums(kind, lo, hi):
            values, table, sum_w, n, factor, col = kind
            nc.tensor.matmul(
                totals[:, :, col + lo : col + hi],
                lhsT=sum_w[:],
                rhs=values[:].rearrange("p k (h s) -> p s (k h)", s=3)[:, :, lo:hi],
                start=True,
                stop=True,
            )

        def means(kind, lo, hi):
            values, table, sum_w, n, factor, col = kind
            total = totals[:, 1, col + lo : col + hi]
            nc.scalar.activation(out=table[:, NEG_MEAN, lo:hi], in_=total, func=ACT.Copy, scale=-n)
            nc.scalar.activation(out=table[:, MEAN_SQ, lo:hi], in_=total, func=ACT.Square, scale=n)

        def mean_of_squares(kind, lo, hi):
            values, table, sum_w, n, factor, col = kind
            nc.vector.tensor_reduce(
                out=table[:, MEAN_OF_SQ, lo:hi],
                in_=totals[:, 0:3:2, col + lo : col + hi].rearrange("p s k -> p k s"),
                axis=AX.X,
                op=ALU.add,
            )

        def no_less(kind, lo, hi):
            row = kind[1][:, MEAN_OF_SQ, lo:hi]
            nc.vector.tensor_tensor(out=row, in0=row, in1=kind[1][:, MEAN_SQ, lo:hi], op=ALU.max)

        def variance(kind, lo, hi):
            table = kind[1]
            nc.vector.tensor_tensor(
                out=table[:, VAR, lo:hi],
                in0=table[:, MEAN_OF_SQ, lo:hi],
                in1=table[:, MEAN_SQ, lo:hi],
                op=ALU.subtract,
            )

        def all_roots_z():
            nc.scalar.activation(out=sz[:, STD, :], in_=sz[:, VAR, :], func=ACT.Sqrt, scale=F_Z)

        def inverses_z():
            nc.vector.tensor_scalar(out=sz[:, STD, :], in0=sz[:, STD, :], scalar1=EPS, scalar2=None, op0=ALU.add)
            nc.vector.reciprocal(out=sz[:, INV_STD, :], in_=sz[:, STD, :])
            nc.vector.tensor_tensor(
                out=sz[:, SHIFT, :], in0=sz[:, NEG_MEAN, :], in1=sz[:, INV_STD, :], op=ALU.mult
            )

        def roots_u(lo, hi):
            row = su[:, STD, lo:hi]
            nc.gpsimd.tensor_tensor(out=row, in0=su[:, VAR, lo:hi], in1=half[:, 0 : hi - lo], op=ALU.pow)
            nc.gpsimd.tensor_scalar(
                out=row, in0=row, scalar1=F_U**0.5, scalar2=EPS, op0=ALU.mult, op1=ALU.add
            )

        def inverses_u(lo, hi):
            nc.vector.reciprocal(out=su[:, INV_STD, lo:hi], in_=su[:, STD, lo:hi])

        tg = {}
        tcd = {}
        ups = {}
        tu = {}

        def standardise(g, bl, d, on_vector):
            if g not in tg:
                tg[g] = tgpool.tile([P, ND * GROUP * P], BF16, name="tg", tag="tg", align_bytes=64)
            k = (GROUP * g + bl) * ND + d
            out = tg[g][:, (d * GROUP + bl) * P : (d * GROUP + bl + 1) * P]
            t = th[g][:, bl, d * P : (d + 1) * P]
            inv_std = sz[:, INV_STD, k : k + 1]
            if on_vector:
                nc.vector.tensor_scalar(
                    out=out,
                    in0=t,
                    scalar1=sz[:, NEG_MEAN, k : k + 1],
                    scalar2=inv_std,
                    op0=ALU.add,
                    op1=ALU.mult,
                )
            else:
                nc.scalar.activation(
                    out=out, in_=t, func=ACT.Identity, scale=inv_std, bias=sz[:, SHIFT, k : k + 1]
                )

        def quantise_t(g):
            cod = tgpool.tile([P, ND * P], U32, name="tcod", tag="tcod", align_bytes=64)
            sc = tgpool.tile([P, ND * P], U8, name="tsc", tag="tsc", align_bytes=64)
            tcd[g] = (cod, sc)
            nc.vector.quantize_mx(out=cod[:].bitcast(FP8X4), scales=sc[:], in_=tg[g][:])

        def matmul_u(g):
            cod, sc = tcd[g]
            u = ps_u.tile([P, ND * ND, NP], F32, name="ups", tag="ups")
            ups[g] = u
            wc, ws = weights[P_XJ]
            for d in range(ND):
                nc.tensor.matmul_mx(
                    out=u[:, ND * d : ND * d + ND, :].rearrange("p k q -> p (k q)"),
                    lhsT=cod[:, d * P : (d + 1) * P].bitcast(FP8X4),
                    lhsT_scale=sc[:, d * P : (d + 1) * P],
                    rhs=wc,
                    rhs_scale=ws,
                    start=True,
                    stop=True,
                )

        def tanh_u(g):
            tu[g] = vpool.tile([P, ND, NP], F32, name="tu", tag="tu")
            nc.scalar.activation(out=tu[g][:], in_=ups[g][:, 0 : ND * ND : ND + 1, :], func=ACT.Tanh)

        def stats_u(g):
            for k in range(ND // 2):
                nc.vector.bn_stats(
                    out=stu[:, g * (ND // 2) + k, :],
                    in_=tu[g][:, 2 * k : 2 * k + 2, :].rearrange("p e q -> p q e"),
                )

        proj = const.tile([P, NG, ND, NP], F32, name="proj")

        def finish(g):
            for d in range(ND):
                k = g * ND + d
                nc.vector.tensor_scalar(
                    out=proj[:, g, d, :],
                    in0=tu[g][:, d, :],
                    scalar1=su[:, NEG_MEAN, k : k + 1],
                    scalar2=su[:, INV_STD, k : k + 1],
                    op0=ALU.add,
                    op1=ALU.mult,
                )
            for bl in range(GROUP):
                nc.sync.dma_start(
                    out=out_0[GROUP * g + bl].rearrange("d n q -> n d q"),
                    in_=proj[NP * bl : NP * bl + NP, g],
                )

        rt = {}
        done = {"product": 0, "maximum": 0, "exponential": 0}

        def product():
            b = done["product"]
            if b == NB:
                return
            done["product"] += 1
            if b % 6 < 4:
                r = ps_xt.tile([P, NI], F32, name="rps", tag="xtb")
            else:
                r = ps_z.tile([P, NI], F32, name="rps", tag="zps")
            rt[b] = r
            cod, sc = xc[b]
            wc, ws = weights[REL_O_XJ]
            nc.tensor.matmul_mx(
                out=r[:],
                lhsT=wc,
                lhsT_scale=ws,
                rhs=cod[:].bitcast(FP8X4),
                rhs_scale=sc[:],
                start=True,
                stop=True,
            )

        def maximum():
            b = done["maximum"]
            if b == NB:
                return
            done["maximum"] += 1
            nc.vector.tensor_reduce(
                out=negmax[:, b : b + 1], in_=rt[b][:], axis=AX.X, op=ALU.max, negate=True
            )

        def exponential():
            b = done["exponential"]
            done["exponential"] += 1
            junk = jpool.tile([P, NI], BF16, name="junk", tag="junk")
            nc.scalar.activation(
                out=junk[:],
                in_=rt[b][:],
                func=ACT.Exp,
                bias=negmax[:, b : b + 1],
                scale=1.0,
                accum_out=expsum[:, b : b + 1],
            )

        def by_item(values):
            turned = ps_u.tile([P, P], F32, name="turned", tag="ups")
            nc.tensor.transpose(turned[:], values[:], ident[:])
            return turned[0:NB, :].rearrange("b (d n) -> b d n", d=ND)

        diff = const.tile([NB, ND, NP], F32, name="diff")

        def below_largest():
            nmt = by_item(negmax)
            least = const.tile([NB, ND], F32, name="least")
            nc.vector.tensor_reduce(out=least[:], in_=nmt, axis=AX.X, op=ALU.min)
            nc.vector.tensor_tensor(
                out=diff[:], in0=least[:].unsqueeze(2).to_broadcast([NB, ND, NP]), in1=nmt, op=ALU.subtract
            )

        def finish_softmax():
            share = const.tile([NB, ND, NP], F32, name="share")
            nc.scalar.activation(out=share[:], in_=diff[:], func=ACT.Exp)
            weighted = const.tile([NB, ND, NP], F32, name="weighted")
            nc.vector.tensor_tensor(out=weighted[:], in0=share[:], in1=by_item(expsum), op=ALU.mult)
            total = const.tile([NB, ND], F32, name="total")
            nc.vector.tensor_reduce(out=total[:], in_=weighted[:], axis=AX.X, op=ALU.add)
            inverse = const.tile([NB, ND], F32, name="inverse")
            nc.vector.reciprocal(out=inverse[:], in_=total[:])
            mass = const.tile([NB, ND, NP], F32, name="mass")
            nc.vector.tensor_tensor(
                out=mass[:],
                in0=weighted[:],
                in1=inverse[:].unsqueeze(2).to_broadcast([NB, ND, NP]),
                op=ALU.mult,
            )
            nc.sync.dma_start(out=out_1[:, :, :], in_=mass[:])

        def chunk_due(s, lag):
            c, rem = divmod(s - lag, CHUNK)
            if rem == CHUNK - 1 and 0 <= c < NB // CHUNK:
                return [(Z, c * CHUNK * ND, (c + 1) * CHUNK * ND)]
            return []

        transposes(0)
        transposes(1)
        for s in range(NB + 3):
            if s == 0:
                copy_half(s, 0, nc.scalar.copy)
                copy_half(s, 1, nc.scalar.copy)
            elif s < NB:
                copy_half(s, 1, nc.scalar.copy)
                if s % V_COPY != 1:
                    copy_half(s, 0, nc.scalar.copy)
            if 0 <= s - 2 < NB:
                tanh_z(s - 2)
            if s == NB + 1:
                load_table(ACT.Sqrt)
            if s == 0:
                quantise_w(O_XJ)
            if 0 <= s - 1 < NB:
                quantise_x(s - 1)
            if s < NB and s % V_COPY == 1:
                copy_half(s, 0, nc.vector.tensor_copy)
            for chunk in chunk_due(s, 6):
                mean_of_squares(*chunk)
            if s == 4:
                quantise_w(REL_O_XJ)
            if s == 5:
                quantise_w(P_XJ)
            if s >= 3:
                stats_z(s - 3)
            for chunk in chunk_due(s, 6):
                no_less(*chunk)
            for chunk in chunk_due(s, 7):
                variance(*chunk)
            if 0 <= s - 1 < NB:
                matmul_z(s - 1)
            if s + 2 < NB:
                transposes(s + 2)
            if s % 2 == 1 and s // 2 + X_PAIRS < NB // 2:
                load_pair(s // 2 + X_PAIRS)
            for chunk in chunk_due(s, 4):
                sums(*chunk)
            for chunk in chunk_due(s, 5):
                means(*chunk)
            for chunk in chunk_due(s, 3):
                place_squares(*chunk)

        last = (Z, (NB - CHUNK) * ND, NB * ND)
        for _ in range(R_FIRST):
            product()
        maximum()
        sums(*last)
        maximum()
        means(*last)
        mean_of_squares(*last)
        no_less(*last)
        variance(*last)
        for _ in range(R_AHEAD - R_FIRST):
            product()
        all_roots_z()
        load_table(ACT.Exp)
        maximum()
        maximum()
        inverses_z()

        work = {}

        def put(q, place, fn, *args):
            work.setdefault((q, place), []).append((fn, args))

        def run(q, place):
            for fn, args in work.get((q, place), []):
                fn(*args)

        for g in range(NG):
            q = SLOTS * g
            for k in range(CALLS):
                on_vector = (CALLS_V * (k + 1) + CALLS // 2) // CALLS > (CALLS_V * k + CALLS // 2) // CALLS
                place = "vector" if on_vector else "scalar"
                put(q + k * SLOTS // CALLS, place, standardise, g, k // ND, k % ND, on_vector)
            put(q + SLOTS, "quantise", quantise_t, g)
            put(q + SLOTS + 1, "u", matmul_u, g)
            put(q + SLOTS + 2, "tanh", tanh_u, g)
            put(q + SLOTS + 3, "after maximum", stats_u, g)
        for lo, hi in ((0, 3), (3, 6), (6, NG)):
            q = SLOTS * (hi - 1) + SLOTS + 5
            cols = (ND * lo, ND * hi)
            put(q, "after maximum", place_squares, U, *cols)
            put(q + 1, "sums", sums, U, *cols)
            put(q + 2, "tanh", means, U, *cols)
            put(q + 3, "before maximum", mean_of_squares, U, *cols)
            put(q + 3, "behind maximum", no_less, U, *cols)
            put(q + 4, "behind maximum", variance, U, *cols)
            put(q + 4, "behind maximum", roots_u, *cols)
            put(q + CHAIN, "before maximum", inverses_u, *cols)
            for g in range(lo, hi):
                put(q + CHAIN, "end", finish, g)

        for q in range(NB):
            product()
            run(q, "sums")
            exponential()
            run(q, "scalar")
            run(q, "before maximum")
            run(q, "quantise")
            maximum()
            run(q, "behind maximum")
            run(q, "vector")
            run(q, "after maximum")
            run(q, "tanh")
            run(q, "u")
            run(q, "end")
            if q == NB - R_AHEAD + 1:
                below_largest()
        finish_softmax()
